import numpy as np
import ml_dtypes


def mxq(x, axis, fmt="e4m3"):
    dtype, down = {"e4m3": (ml_dtypes.float8_e4m3fn, 7), "e5m2": (ml_dtypes.float8_e5m2, 14)}[fmt]
    v = np.moveaxis(np.asarray(x, np.float32).astype(ml_dtypes.bfloat16).astype(np.float64), axis, -1)
    blocks = v.reshape(v.shape[:-1] + (-1, 32))
    amax = np.abs(blocks).max(-1, keepdims=True)
    byte = np.maximum(np.where(amax > 0, np.frexp(amax)[1] - 1 + 127, 0) - down, 1)
    scale = np.exp2(byte - 127.0)
    codes = (blocks / scale).astype(np.float32).astype(dtype).astype(np.float64)
    return np.moveaxis((codes * scale).reshape(v.shape), -1, axis)


WIDE = False


def mx_kscale(k, group=512):
    if not WIDE:
        return np.ones(k)
    levels = np.array([10, -10, 5, -5, 0])
    if group != 512:
        return np.exp2(np.random.permutation(np.resize(levels, k // group))).repeat(group)
    if k % 512:
        return np.exp2(np.random.permutation(np.resize(levels, k // 32))).repeat(32)
    a = np.empty((k // 512, 16))
    for p in range(k // 512):
        a[p, :8] = np.random.permutation(np.resize(levels, 8))
        for g in range(8):
            far = levels[np.abs(levels - a[p, g]) >= 10]
            a[p, g + 8] = far[np.random.randint(len(far))]
    return np.exp2(a.ravel()).repeat(32)


BF16 = ml_dtypes.bfloat16


def bf(x):
    return np.asarray(x, np.float32).astype(BF16)


def f64(x):
    return np.asarray(x).astype(np.float64)


B, H, W, C, NS = 2, 2, 1024, 512, 2
WIN = W // NS
SHIFT = WIN // 2


def windows(x, b, h, w, n):
    x = f64(x)
    c = x.shape[-1]
    x = np.roll(x.reshape(b * h, w, c), -(w // n // 2), axis=1)
    return x.reshape(b * h, n, w // n, c)


def unwindows(x, b, h, w, n):
    c = x.shape[-1]
    x = np.roll(x.reshape(b * h, w, c), w // n // 2, axis=1)
    return x.reshape(b, h * w, c)


def setup_inputs():
    s = mx_kscale(WIN, 128)
    u = mx_kscale(C, 128)
    q = bf(np.random.standard_normal((B, H * W, C)))
    k = bf(np.random.standard_normal((B, H * W, C)))
    v0 = bf(np.random.standard_normal((B, H * W, C)) * 2.0)
    m0 = bf(np.random.standard_normal((NS, WIN, WIN)))
    g = bf(np.random.standard_normal((B, H * W, C)) * np.exp2(np.random.randint(-6, 1, (B, H * W, 1))) * 16.0 * u)
    scores = windows(q, B, H, W, NS) @ windows(k, B, H, W, NS).transpose(0, 1, 3, 2) / C ** 0.5
    row_max = (scores + f64(m0)[None]).max(-1)
    return {"q": q, "k": k,
            "v": bf(f64(v0) / u),
            "attn_mask": bf(f64(m0) + np.log(s)[None, :, None]),
            "h": H, "w": W, "num_splits": NS,
            "scores": np.asarray(scores, np.float32),
            "row_max": np.asarray(row_max, np.float32),
            "grad_out": g}


def reference(q, k, v, attn_mask, h, w, num_splits, scores, row_max, grad_out):
    b = v.shape[0]
    vs = windows(v, b, h, w, num_splits)
    gs = windows(grad_out, b, h, w, num_splits)
    e = np.exp(f64(scores) + f64(attn_mask)[None] - f64(row_max)[..., None])
    z = e.sum(-1, keepdims=True)
    dz = gs / z
    dvs = mxq(e, 2, "e4m3").transpose(0, 1, 3, 2) @ mxq(dz, 2, "e5m2")
    de = mxq(dz, 3, "e5m2") @ mxq(vs, 3, "e4m3").transpose(0, 1, 3, 2)
    ds = e * (de - (e * de).sum(-1, keepdims=True) / z)
    return unwindows(dvs, b, h, w, num_splits), ds.sum(0)

@@ -1,0 +1,364 @@
+from contextlib import ExitStack
+
+import concourse.mybir as mybir
+from concourse.masks import make_identity
+
+F32 = mybir.dt.float32
+BF16 = mybir.dt.bfloat16
+U32 = mybir.dt.uint32
+U8 = mybir.dt.uint8
+E4M3X4 = mybir.dt.float8_e4m3fn_x4
+E5M2X4 = mybir.dt.float8_e5m2_x4
+ADD = mybir.AluOpType.add
+MULT = mybir.AluOpType.mult
+EXP = mybir.ActivationFunctionType.Exp
+
+P = 128
+J = 4
+WIN = 512
+C = 512
+ROWS = 4
+SPLITS = 2
+
+FLOPS = 2 * ROWS * SPLITS * 2 * WIN * WIN * C
+BYTES = 4 * ROWS * SPLITS * WIN * WIN + 2 * 2 * (ROWS * SPLITS * WIN * C) + 2 * SPLITS * WIN * WIN + 4 * ROWS * SPLITS * WIN * C + 4 * SPLITS * WIN * WIN
+
+V_FIRST = False
+SUBTRACT = mybir.AluOpType.subtract
+PE_ROWS = ((4, 4, 4, 0), (3, 3, 3, 0))
+G_ACC_UNTIL = 7
+E_COLS_ON_VECTOR = (384,) * 8
+
+DZ_COLS_ON_VECTOR = (0, 0, 0, 0, 0, 0, 0, 0)
+V_ON_VECTOR = ()
+BANK_BUFS, DE_BUFS, SUM_BUFS = 3, 2, 3
+G_TILES = (0, 3, 3, 3, 3, 3, 3, 3)
+
+
+def tile_single_head_split_window_attention_1d_v_kernel(
+    tc, q, k, v, attn_mask, h, w, num_splits, scores, row_max, grad_out, out_0, out_1
+):
+    nc = tc.nc
+    assert (w, num_splits) == (SPLITS * WIN, SPLITS)
+    steps = [(n, r) for n in range(SPLITS) for r in range(ROWS)]
+    last = len(steps) - 1
+
+    with ExitStack() as ctx:
+        keep = ctx.enter_context(tc.tile_pool(name="keep", bufs=1))
+        io = ctx.enter_context(tc.tile_pool(name="io", bufs=1))
+        work = ctx.enter_context(tc.tile_pool(name="work", bufs=2))
+        small = ctx.enter_context(tc.tile_pool(name="small", bufs=4))
+        psum = ctx.enter_context(tc.psum_pool(name="psum", bufs=1))
+
+        ident = keep.tile([P, P], F32, name="ident")
+        warm = keep.tile([P, 1], F32, name="warm")
+        rmax = keep.tile([P, len(steps), 2 * J], F32, name="rmax")
+        neg_max = keep.tile([P, len(steps), J], F32, name="neg_max")
+        mask = [keep.tile([P, J, WIN], BF16, name="mask%d" % n) for n in range(SPLITS)]
+        acc = [keep.tile([P, J, WIN], F32, name="acc%d" % n) for n in range(SPLITS)]
+        tiles = [dict() for s in steps]
+        sums = {}
+
+        def image(x, r):
+            return x[r // h]
+
+        def spans(n, r):
+            first = (r % h) * w
+            start = n * WIN + WIN // 2
+            if start + WIN <= w:
+                return [(0, first + start, WIN)]
+            head = w - start
+            return [(0, first + start, head), (head, first, WIN - head)]
+
+        def load_scores(i, halves):
+            n, r = steps[i]
+            t = io.tile([P, J, WIN], F32, name="e", bufs=6)
+            tiles[i]["e"] = t
+            src = scores[r, n].rearrange("(p j) k -> p j k", j=J)
+            for a in range(0, J, J // halves):
+                nc.sync.dma_start(out=t[:, a : a + J // halves, :], in_=src[:, a : a + J // halves, :])
+                if r == 0:
+                    msrc = attn_mask[n].rearrange("(p j) k -> p j k", j=J)
+                    nc.sync.dma_start(out=mask[n][:, a : a + J // halves, :], in_=msrc[:, a : a + J // halves, :])
+
+        def late_loads(i):
+            if i >= 5:
+                load_scores(i, 1)
+                load_grad(i)
+                load_v(i)
+
+        def load_grad(i):
+            n, r = steps[i]
+            t = io.tile([P, J, C], BF16, name="g", bufs=5)
+            tiles[i]["g"] = t
+            for win0, x0, rows in spans(n, r):
+                src = image(grad_out, r)[x0 : x0 + rows, :].rearrange("(p j) c -> p j c", j=J)
+                nc.sync.dma_start(out=t[win0 // J : (win0 + rows) // J, :, :], in_=src)
+
+        def load_v(i):
+            n, r = steps[i]
+            t = io.tile([P, J, C], BF16, name="v", bufs=5)
+            tiles[i]["v"] = t
+            for win0, x0, rows in spans(n, r):
+                src = image(v, r)[x0 : x0 + rows, :].rearrange("(t p) c -> p t c", p=P)
+                nc.sync.dma_start(out=t[:, win0 // P : (win0 + rows) // P, :], in_=src)
+
+        def add_mask(i):
+            e, m = tiles[i]["e"], mask[steps[i][0]]
+            mine = J - G_TILES[i]
+            step = 1 if i == 0 else max(mine, 1)
+            for a in range(0, mine, step):
+                nc.vector.tensor_tensor(out=e[:, a : a + step, :], in0=e[:, a : a + step, :], in1=m[:, a : a + step, :], op=ADD)
+
+        def add_mask_g(i, j):
+            if j >= J - G_TILES[i]:
+                e, m = tiles[i]["e"], mask[steps[i][0]]
+                nc.gpsimd.tensor_tensor(out=e[:, j, :], in0=e[:, j, :], in1=m[:, j, :], op=ADD)
+
+        def exponential(i, j):
+            if j == 0:
+                tiles[i]["z"] = small.tile([P, J], F32, name="z")
+            e = tiles[i]["e"]
+            nc.scalar.activation(
+                out=e[:, j, :], in_=e[:, j, :], func=EXP, bias=neg_max[:, i, j : j + 1], accum_out=tiles[i]["z"][:, j : j + 1]
+            )
+
+        def invert(i):
+            tiles[i]["rz"] = small.tile([P, J], F32, name="rz")
+            nc.vector.reciprocal(out=tiles[i]["rz"][:], in_=tiles[i]["z"][:])
+
+        def scale(i):
+            tiles[i]["dz"] = work.tile([P, J, C], BF16, name="dz", bufs=3, align_bytes=64)
+            for j in range(J):
+                nc.vector.tensor_scalar(
+                    out=tiles[i]["dz"][:, j, :], in0=tiles[i]["g"][:, j, :], scalar1=tiles[i]["rz"][:, j : j + 1], scalar2=None, op0=MULT
+                )
+
+        def four_by_four(dst, src, cols):
+            return dict(
+                out=dst[:, cols, :].rearrange("p (c i) j -> p c j i", i=4),
+                in_=src[:, :, cols].rearrange("p j (c i) -> p c j i", i=4),
+            )
+
+        def interleave_e_v(i):
+            tiles[i]["ev"] = work.tile([P, 2, WIN, J], BF16, name="ev", bufs=3, align_bytes=64)
+            tiles[i]["e_il"] = tiles[i]["ev"][:, 0]
+            tiles[i]["v_t"] = tiles[i]["ev"][:, 1]
+            if E_COLS_ON_VECTOR[i]:
+                nc.vector.tensor_copy(**four_by_four(tiles[i]["e_il"], tiles[i]["e"], slice(0, E_COLS_ON_VECTOR[i])))
+
+        def interleave_e_s(i):
+            if E_COLS_ON_VECTOR[i] < WIN:
+                nc.scalar.copy(**four_by_four(tiles[i]["e_il"], tiles[i]["e"], slice(E_COLS_ON_VECTOR[i], WIN)))
+
+        def interleave_dz(i):
+            tiles[i]["dz_il"] = work.tile([P, C, J], BF16, name="dz_il", bufs=3, align_bytes=64)
+            if DZ_COLS_ON_VECTOR[i] < C:
+                nc.scalar.copy(**four_by_four(tiles[i]["dz_il"], tiles[i]["dz"], slice(0, C - DZ_COLS_ON_VECTOR[i])))
+
+        def interleave_dz_v(i):
+            if DZ_COLS_ON_VECTOR[i]:
+                nc.vector.tensor_copy(**four_by_four(tiles[i]["dz_il"], tiles[i]["dz"], slice(C - DZ_COLS_ON_VECTOR[i], C)))
+
+        def quantise(i, name, src, fmt):
+            codes = work.tile([P, 512], U32, name=name + "_q", align_bytes=64)
+            scl = work.tile([P, 512], U8, name=name + "_s", align_bytes=64)
+            tiles[i][name + "_q"] = codes[:].bitcast(fmt)
+            tiles[i][name + "_s"] = scl
+            nc.vector.quantize_mx(out=codes[:].bitcast(fmt), scales=scl[:], in_=tiles[i][src][:].rearrange("p a b -> p (a b)"))
+
+        def quantise_ev(i):
+            codes = work.tile([P, 2, 512], U32, name="ev_q", align_bytes=64)
+            scl = work.tile([P, 2, 512], U8, name="ev_s", align_bytes=64)
+            t = tiles[i]
+            nc.vector.quantize_mx(
+                out=codes[:].rearrange("p o x -> p (o x)").bitcast(E4M3X4),
+                scales=scl[:].rearrange("p o x -> p (o x)"),
+                in_=t["ev"][:].rearrange("p o x j -> p (o x j)"),
+            )
+            t["e_q"], t["e_s"] = codes[:, 0, :].bitcast(E4M3X4), scl[:, 0, :]
+            t["vt_q"], t["vt_s"] = codes[:, 1, :].bitcast(E4M3X4), scl[:, 1, :]
+
+        def turn(i, name, b):
+            words = tiles[i][name][:].rearrange("p a c -> p (a c)").bitcast(F32).rearrange("p (a c) -> p a c", a=J)
+            ps = psum.tile([P, 2, 2, P], F32, name="turn", tag="bank", bufs=BANK_BUFS)
+            tiles[i][name, b] = ps
+            for a in range(2):
+                for u in range(2):
+                    nc.tensor.transpose(ps[:, a, u, :], words[:, 2 * b + a, u : C // 2 : 2], ident[:])
+
+        def unload(i, name, b):
+            if b == 0 and name == "dz":
+                tiles[i]["dz_t"] = work.tile([P, WIN, J], BF16, name="dz_t", bufs=3, align_bytes=64)
+            words = tiles[i][name + "_t"][:].rearrange("p x j -> p (x j)").bitcast(F32)
+            words = words.rearrange("p (b a x u) -> p b a x u", b=2, a=2, u=2)
+            src = tiles[i][name, b][:].rearrange("p a u x -> p a x u")
+            if name == "v" and (i, b) in V_ON_VECTOR:
+                nc.vector.tensor_copy(out=words[:, b], in_=src)
+            else:
+                nc.scalar.copy(out=words[:, b], in_=src)
+
+        def multiply_de(i, j):
+            t = tiles[i]
+            ps = psum.tile([P, WIN], F32, name="de", bufs=DE_BUFS)
+            t["de", j] = ps
+            cols = slice(P * j, P * (j + 1))
+            nc.tensor.matmul_mx(
+                out=ps[:], lhsT=t["dzt_q"][:, cols], lhsT_scale=t["dzt_s"][:, cols], rhs=t["vt_q"], rhs_scale=t["vt_s"],
+                start=True, stop=True,
+            )
+
+        def multiply_dv(i, m):
+            t = tiles[i]
+            ps = psum.tile([P, C], F32, name="dv", tag="bank", bufs=BANK_BUFS)
+            t["dv", m] = ps
+            cols = slice(P * m, P * (m + 1))
+            nc.tensor.matmul_mx(
+                out=ps[:], lhsT=t["e_q"][:, cols], lhsT_scale=t["e_s"][:, cols], rhs=t["dz_q"], rhs_scale=t["dz_s"][:],
+                start=True, stop=True,
+            )
+
+        def empty_dv(i, m):
+            n, r = steps[i]
+            if m == 0:
+                tiles[i]["dv_sb"] = work.tile([P, J, C], F32, name="dv_sb")
+            sb = tiles[i]["dv_sb"]
+            nc.scalar.copy(out=sb[:, m, :], in_=tiles[i]["dv", m][:])
+            if m % 2:
+                x0 = [x0 + P * (m - 1) - win0 for win0, x0, rows in spans(n, r) if win0 <= P * (m - 1) < win0 + rows][0]
+                dst = image(out_0, r)[x0 : x0 + 2 * P, :].rearrange("(t p) c -> p t c", p=P)
+                nc.sync.dma_start(out=dst, in_=sb[:, m - 1 : m + 1, :])
+
+        def weigh(i, j):
+            if j == 0:
+                tiles[i]["ds"] = work.tile([P, J, WIN], F32, name="ds")
+                tiles[i]["dot"] = small.tile([P, J], F32, name="dot")
+            t = tiles[i]
+            waste = work.tile([P, WIN], F32, name="waste")
+            nc.vector.scalar_tensor_tensor(
+                out=waste[:], in0=t["de", j][:], scalar=t["rz"][:, j : j + 1], in1=t["e"][:, j, :], op0=MULT, op1=MULT,
+                accum_out=t["dot"][:, j : j + 1],
+            )
+
+        def subtract(i, j):
+            n, r = steps[i]
+            t = tiles[i]
+            dst = acc[n] if r == 0 and PE_ROWS[n][j] == 0 else t["ds"]
+            nc.vector.scalar_tensor_tensor(
+                out=dst[:, j, :], in0=t["de", j][:], scalar=t["dot"][:, j : j + 1], in1=t["e"][:, j, :], op0=SUBTRACT, op1=MULT
+            )
+
+        def sum_on_tensor(i, j):
+            n, r = steps[i]
+            if r < PE_ROWS[n][j]:
+                if r == 0:
+                    sums[n, j] = psum.tile([P, WIN], F32, name="sum", bufs=SUM_BUFS)
+                nc.tensor.matmul(out=sums[n, j][:], lhsT=ident[:], rhs=tiles[i]["ds"][:, j, :], start=(r == 0), stop=(r == PE_ROWS[n][j] - 1))
+
+        def accumulate(i, j):
+            n, r = steps[i]
+            if PE_ROWS[n][j] == 0 and r > 0:
+                engine = nc.gpsimd if i < G_ACC_UNTIL else nc.vector
+                engine.tensor_tensor(out=acc[n][:, j, :], in0=acc[n][:, j, :], in1=tiles[i]["ds"][:, j, :], op=ADD)
+                if r == ROWS - 1:
+                    store_sum(n, j)
+
+        def store_sum(n, j):
+            nc.sync.dma_start(out=out_1[n].rearrange("(p j) k -> p j k", j=J)[:, j, :], in_=acc[n][:, j, :])
+
+        def empty_sum(i, j):
+            n, r = steps[i]
+            if r == ROWS - 1 and PE_ROWS[n][j] == ROWS:
+                nc.scalar.copy(out=acc[n][:, j, :], in_=sums[n, j][:])
+                store_sum(n, j)
+
+        def merge(i, j):
+            n, r = steps[i]
+            if r == ROWS - 1 and PE_ROWS[n][j] == ROWS - 1:
+                nc.vector.tensor_tensor(out=acc[n][:, j, :], in0=sums[n, j][:], in1=tiles[i]["ds"][:, j, :], op=ADD)
+                store_sum(n, j)
+
+        make_identity(nc, ident[:])
+        nc.vector.memset(warm[:], 0.0)
+        nc.scalar.activation(out=warm[:], in_=warm[:], func=EXP)
+        with tc.manual_schedule():
+            for a, b in ((0, 1), (1, 4), (4, 5), (5, 8)):
+                n, r0 = steps[a]
+                src = row_max[r0 : r0 + b - a, n].rearrange("r (p j) -> p r j", j=J)
+                nc.scalar.dma_start(out=rmax[:, a:b, 0:J], in_=src)
+            for a, b in ((0, 1), (1, 8)):
+                nc.gpsimd.tensor_scalar(out=neg_max[:, a:b, :], in0=rmax[:, a:b, 0:J], scalar1=-1.0, scalar2=0.0, op0=MULT, op1=ADD)
+            if V_FIRST:
+                load_v(0)
+            load_scores(0, 4)
+            if not V_FIRST:
+                load_v(0)
+            load_grad(0)
+            for i in range(1, 5):
+                load_scores(i, 1)
+                load_grad(i)
+                load_v(i)
+
+            order = (
+                (sum_on_tensor, -1, 1),
+                (subtract, -1, 3),
+                (sum_on_tensor, -2, 2),
+                (multiply_de, 0, 0),
+                (late_loads, 3),
+                (interleave_e_v, 1),
+                (unload, 1, "v", 0),
+                (multiply_dv, -1, 3),
+                (empty_sum, -2, 0),
+                (accumulate, -2, 3),
+                (interleave_dz, 0),
+                (multiply_de, 0, 1),
+                (empty_sum, -1, 1),
+                (turn, 1, "v", 1),
+                (add_mask_g, 2, 3),
+                (scale, 1),
+                (turn, 1, "dz", 0),
+                (sum_on_tensor, -1, 0),
+                (add_mask, 2),
+                (weigh, 0, 0),
+                (empty_dv, -1, 3),
+                (interleave_e_s, 1),
+                (weigh, 0, 1),
+                (add_mask_g, 2, 2),
+                (add_mask_g, 2, 1),
+                (quantise, 0, "dz", "dz_il", E5M2X4),
+                (turn, 1, "dz", 1),
+                (exponential, 2, 0),
+                (unload, 1, "v", 1),
+                (multiply_dv, 0, 0),
+                (subtract, 0, 0),
+                (unload, 1, "dz", 0),
+                (subtract, 0, 1),
+                (quantise_ev, 1),
+                (exponential, 2, 2),
+                (merge, 0, 0),
+                (unload, 1, "dz", 1),
+                (merge, -1, 2),
+                (multiply_de, 0, 2),
+                (empty_dv, 0, 0),
+                (multiply_dv, 0, 2),
+                (multiply_de, 0, 3),
+                (exponential, 2, 3),
+                (multiply_dv, 0, 1),
+                (merge, 0, 1),
+                (turn, 2, "v", 0),
+                (quantise, 1, "dzt", "dz_t", E5M2X4),
+                (interleave_dz_v, -2),
+                (weigh, 0, 2),
+                (exponential, 2, 1),
+                (empty_sum, -2, 2),
+                (add_mask_g, 2, 0),
+                (empty_dv, 0, 2),
+                (weigh, 0, 3),
+                (empty_dv, 0, 1),
+                (invert, 2),
+                (subtract, 0, 2),
+            )
+            for t in range(-3, last + 4):
+                for op, ahead, *args in order:
+                    if 0 <= t + ahead <= last:
+                        op(t + ahead, *args)

@@ -11,6 +11,7 @@ E4M3X4 = mybir.dt.float8_e4m3fn_x4
 E5M2X4 = mybir.dt.float8_e5m2_x4
 ADD = mybir.AluOpType.add
 MULT = mybir.AluOpType.mult
+SUBTRACT = mybir.AluOpType.subtract
 EXP = mybir.ActivationFunctionType.Exp
 
 P = 128
@@ -19,20 +20,10 @@ WIN = 512
 C = 512
 ROWS = 4
 SPLITS = 2
+E_ON_SCALAR = 64
 
 FLOPS = 2 * ROWS * SPLITS * 2 * WIN * WIN * C
 BYTES = 4 * ROWS * SPLITS * WIN * WIN + 2 * 2 * (ROWS * SPLITS * WIN * C) + 2 * SPLITS * WIN * WIN + 4 * ROWS * SPLITS * WIN * C + 4 * SPLITS * WIN * WIN
-
-V_FIRST = False
-SUBTRACT = mybir.AluOpType.subtract
-PE_ROWS = ((4, 4, 4, 0), (3, 3, 3, 0))
-G_ACC_UNTIL = 7
-E_COLS_ON_VECTOR = (384,) * 8
-
-DZ_COLS_ON_VECTOR = (0, 0, 0, 0, 0, 0, 0, 0)
-V_ON_VECTOR = ()
-BANK_BUFS, DE_BUFS, SUM_BUFS = 3, 2, 3
-G_TILES = (0, 3, 3, 3, 3, 3, 3, 3)
 
 
 def tile_single_head_split_window_attention_1d_v_kernel(
@@ -45,7 +36,6 @@ def tile_single_head_split_window_attention_1d_v_kernel(
 
     with ExitStack() as ctx:
         keep = ctx.enter_context(tc.tile_pool(name="keep", bufs=1))
-        io = ctx.enter_context(tc.tile_pool(name="io", bufs=1))
         work = ctx.enter_context(tc.tile_pool(name="work", bufs=2))
         small = ctx.enter_context(tc.tile_pool(name="small", bufs=4))
         psum = ctx.enter_context(tc.psum_pool(name="psum", bufs=1))
@@ -55,8 +45,8 @@ def tile_single_head_split_window_attention_1d_v_kernel(
         rmax = keep.tile([P, len(steps), 2 * J], F32, name="rmax")
         neg_max = keep.tile([P, len(steps), J], F32, name="neg_max")
         mask = [keep.tile([P, J, WIN], BF16, name="mask%d" % n) for n in range(SPLITS)]
-        acc = [keep.tile([P, J, WIN], F32, name="acc%d" % n) for n in range(SPLITS)]
         tiles = [dict() for s in steps]
+        units = [dict() for u in range(2 * len(steps))]
         sums = {}
 
         def image(x, r):
@@ -70,68 +60,69 @@ def tile_single_head_split_window_attention_1d_v_kernel(
             head = w - start
             return [(0, first + start, head), (head, first, WIN - head)]
 
-        def load_scores(i, halves):
+        def load_scores(i, a, b):
             n, r = steps[i]
-            t = io.tile([P, J, WIN], F32, name="e", bufs=6)
-            tiles[i]["e"] = t
+            if a == 0:
+                tiles[i]["e"] = keep.tile([P, J, WIN], F32, name="e%d" % i)
             src = scores[r, n].rearrange("(p j) k -> p j k", j=J)
-            for a in range(0, J, J // halves):
-                nc.sync.dma_start(out=t[:, a : a + J // halves, :], in_=src[:, a : a + J // halves, :])
-                if r == 0:
-                    msrc = attn_mask[n].rearrange("(p j) k -> p j k", j=J)
-                    nc.sync.dma_start(out=mask[n][:, a : a + J // halves, :], in_=msrc[:, a : a + J // halves, :])
+            nc.sync.dma_start(out=tiles[i]["e"][:, a:b, :], in_=src[:, a:b, :])
+            if r == 0:
+                msrc = attn_mask[n].rearrange("(p j) k -> p j k", j=J)
+                nc.sync.dma_start(out=mask[n][:, a:b, :], in_=msrc[:, a:b, :])
 
-        def late_loads(i):
-            if i >= 5:
-                load_scores(i, 1)
-                load_grad(i)
-                load_v(i)
-
-        def load_grad(i):
+        def load_grad(i, a, b):
             n, r = steps[i]
-            t = io.tile([P, J, C], BF16, name="g", bufs=5)
-            tiles[i]["g"] = t
+            if a == 0:
+                tiles[i]["g"] = keep.tile([P, J, C], BF16, name="g%d" % i)
             for win0, x0, rows in spans(n, r):
                 src = image(grad_out, r)[x0 : x0 + rows, :].rearrange("(p j) c -> p j c", j=J)
-                nc.sync.dma_start(out=t[win0 // J : (win0 + rows) // J, :, :], in_=src)
+                nc.sync.dma_start(out=tiles[i]["g"][win0 // J : (win0 + rows) // J, a:b, :], in_=src[:, a:b, :])
 
         def load_v(i):
             n, r = steps[i]
-            t = io.tile([P, J, C], BF16, name="v", bufs=5)
+            t = keep.tile([P, J, C], BF16, name="v%d" % i)
             tiles[i]["v"] = t
             for win0, x0, rows in spans(n, r):
                 src = image(v, r)[x0 : x0 + rows, :].rearrange("(t p) c -> p t c", p=P)
                 nc.sync.dma_start(out=t[:, win0 // P : (win0 + rows) // P, :], in_=src)
 
-        def add_mask(i):
+        def add_mask_vector(i, a, b):
             e, m = tiles[i]["e"], mask[steps[i][0]]
-            mine = J - G_TILES[i]
-            step = 1 if i == 0 else max(mine, 1)
-            for a in range(0, mine, step):
-                nc.vector.tensor_tensor(out=e[:, a : a + step, :], in0=e[:, a : a + step, :], in1=m[:, a : a + step, :], op=ADD)
+            nc.vector.tensor_tensor(out=e[:, a:b, :], in0=e[:, a:b, :], in1=m[:, a:b, :], op=ADD)
+            for j in range(a, b):
+                tiles[i]["t", j] = e[:, j, :]
 
-        def add_mask_g(i, j):
-            if j >= J - G_TILES[i]:
-                e, m = tiles[i]["e"], mask[steps[i][0]]
-                nc.gpsimd.tensor_tensor(out=e[:, j, :], in0=e[:, j, :], in1=m[:, j, :], op=ADD)
+        def add_mask_gpsimd(u, tag):
+            i, half = divmod(u, 2)
+            e, m = tiles[i]["e"], mask[steps[i][0]]
+            t = work.tile([P, 2, WIN], F32, name="t", tag=tag, bufs=1, align_bytes=64)
+            js = slice(2 * half, 2 * half + 2)
+            nc.gpsimd.tensor_tensor(out=t[:], in0=e[:, js, :], in1=m[:, js, :], op=ADD)
+            for a in range(2):
+                tiles[i]["t", 2 * half + a] = t[:, a, :]
 
-        def exponential(i, j):
-            if j == 0:
-                tiles[i]["z"] = small.tile([P, J], F32, name="z")
-            e = tiles[i]["e"]
+        def exponential(u, a):
+            i, half = divmod(u, 2)
+            j = 2 * half + a
+            if a == 0:
+                units[u]["z"] = small.tile([P, 2], F32, name="z")
             nc.scalar.activation(
-                out=e[:, j, :], in_=e[:, j, :], func=EXP, bias=neg_max[:, i, j : j + 1], accum_out=tiles[i]["z"][:, j : j + 1]
+                out=tiles[i]["e"][:, j, :], in_=tiles[i]["t", j], func=EXP, bias=neg_max[:, i, j : j + 1],
+                accum_out=units[u]["z"][:, a : a + 1],
             )
 
-        def invert(i):
-            tiles[i]["rz"] = small.tile([P, J], F32, name="rz")
-            nc.vector.reciprocal(out=tiles[i]["rz"][:], in_=tiles[i]["z"][:])
+        def invert(u):
+            units[u]["rz"] = small.tile([P, 2], F32, name="rz")
+            nc.vector.reciprocal(out=units[u]["rz"][:], in_=units[u]["z"][:])
 
-        def scale(i):
-            tiles[i]["dz"] = work.tile([P, J, C], BF16, name="dz", bufs=3, align_bytes=64)
-            for j in range(J):
+        def scale(u):
+            i, half = divmod(u, 2)
+            if half == 0:
+                tiles[i]["dz"] = work.tile([P, J, C], BF16, name="dz", align_bytes=64)
+            for a in range(2):
+                j = 2 * half + a
                 nc.vector.tensor_scalar(
-                    out=tiles[i]["dz"][:, j, :], in0=tiles[i]["g"][:, j, :], scalar1=tiles[i]["rz"][:, j : j + 1], scalar2=None, op0=MULT
+                    out=tiles[i]["dz"][:, j, :], in0=tiles[i]["g"][:, j, :], scalar1=units[u]["rz"][:, a : a + 1], scalar2=None, op0=MULT
                 )
 
         def four_by_four(dst, src, cols):
@@ -140,81 +131,75 @@ def tile_single_head_split_window_attention_1d_v_kernel(
                 in_=src[:, :, cols].rearrange("p j (c i) -> p c j i", i=4),
             )
 
-        def interleave_e_v(i):
-            tiles[i]["ev"] = work.tile([P, 2, WIN, J], BF16, name="ev", bufs=3, align_bytes=64)
-            tiles[i]["e_il"] = tiles[i]["ev"][:, 0]
-            tiles[i]["v_t"] = tiles[i]["ev"][:, 1]
-            if E_COLS_ON_VECTOR[i]:
-                nc.vector.tensor_copy(**four_by_four(tiles[i]["e_il"], tiles[i]["e"], slice(0, E_COLS_ON_VECTOR[i])))
+        def interleave_e_scalar(i):
+            tiles[i]["e_il"] = work.tile([P, WIN, J], BF16, name="e_il", tag="e_il%d" % (i % 2), bufs=1, align_bytes=64)
+            nc.scalar.copy(**four_by_four(tiles[i]["e_il"], tiles[i]["e"], slice(0, E_ON_SCALAR)))
 
-        def interleave_e_s(i):
-            if E_COLS_ON_VECTOR[i] < WIN:
-                nc.scalar.copy(**four_by_four(tiles[i]["e_il"], tiles[i]["e"], slice(E_COLS_ON_VECTOR[i], WIN)))
+        def interleave_e_vector(i):
+            nc.vector.tensor_copy(**four_by_four(tiles[i]["e_il"], tiles[i]["e"], slice(E_ON_SCALAR, WIN)))
 
-        def interleave_dz(i):
-            tiles[i]["dz_il"] = work.tile([P, C, J], BF16, name="dz_il", bufs=3, align_bytes=64)
-            if DZ_COLS_ON_VECTOR[i] < C:
-                nc.scalar.copy(**four_by_four(tiles[i]["dz_il"], tiles[i]["dz"], slice(0, C - DZ_COLS_ON_VECTOR[i])))
+        def interleave_dz(i, half):
+            if half == 0:
+                tiles[i]["dz_il"] = work.tile([P, C, J], BF16, name="dz_il", tag="dz_il%d" % (i % 2), bufs=1, align_bytes=64)
+            nc.scalar.copy(**four_by_four(tiles[i]["dz_il"], tiles[i]["dz"], slice(half * C // 2, (half + 1) * C // 2)))
 
-        def interleave_dz_v(i):
-            if DZ_COLS_ON_VECTOR[i]:
-                nc.vector.tensor_copy(**four_by_four(tiles[i]["dz_il"], tiles[i]["dz"], slice(C - DZ_COLS_ON_VECTOR[i], C)))
+        def quantise(held, name, fmt):
+            src = held[name][:].rearrange("p a b -> p (a b)")
+            width = src.shape[1] // J
+            codes = work.tile([P, width], U32, name=name + "_q", align_bytes=64)
+            scl = work.tile([P, width], U8, name=name + "_s", align_bytes=64)
+            held[name, "q"] = codes[:].bitcast(fmt)
+            held[name, "s"] = scl
+            nc.vector.quantize_mx(out=codes[:].bitcast(fmt), scales=scl[:], in_=src)
 
-        def quantise(i, name, src, fmt):
-            codes = work.tile([P, 512], U32, name=name + "_q", align_bytes=64)
-            scl = work.tile([P, 512], U8, name=name + "_s", align_bytes=64)
-            tiles[i][name + "_q"] = codes[:].bitcast(fmt)
-            tiles[i][name + "_s"] = scl
-            nc.vector.quantize_mx(out=codes[:].bitcast(fmt), scales=scl[:], in_=tiles[i][src][:].rearrange("p a b -> p (a b)"))
+        def quantise_step(i, name, fmt):
+            quantise(tiles[i], name, fmt)
 
-        def quantise_ev(i):
-            codes = work.tile([P, 2, 512], U32, name="ev_q", align_bytes=64)
-            scl = work.tile([P, 2, 512], U8, name="ev_s", align_bytes=64)
-            t = tiles[i]
-            nc.vector.quantize_mx(
-                out=codes[:].rearrange("p o x -> p (o x)").bitcast(E4M3X4),
-                scales=scl[:].rearrange("p o x -> p (o x)"),
-                in_=t["ev"][:].rearrange("p o x j -> p (o x j)"),
-            )
-            t["e_q"], t["e_s"] = codes[:, 0, :].bitcast(E4M3X4), scl[:, 0, :]
-            t["vt_q"], t["vt_s"] = codes[:, 1, :].bitcast(E4M3X4), scl[:, 1, :]
+        def quantise_dz_t(u):
+            quantise(units[u], "dz_t", E5M2X4)
 
         def turn(i, name, b):
             words = tiles[i][name][:].rearrange("p a c -> p (a c)").bitcast(F32).rearrange("p (a c) -> p a c", a=J)
-            ps = psum.tile([P, 2, 2, P], F32, name="turn", tag="bank", bufs=BANK_BUFS)
+            ps = psum.tile([P, 2, 2, P], F32, name="turn", tag="bank", bufs=2)
             tiles[i][name, b] = ps
             for a in range(2):
                 for u in range(2):
                     nc.tensor.transpose(ps[:, a, u, :], words[:, 2 * b + a, u : C // 2 : 2], ident[:])
 
-        def unload(i, name, b):
-            if b == 0 and name == "dz":
-                tiles[i]["dz_t"] = work.tile([P, WIN, J], BF16, name="dz_t", bufs=3, align_bytes=64)
-            words = tiles[i][name + "_t"][:].rearrange("p x j -> p (x j)").bitcast(F32)
-            words = words.rearrange("p (b a x u) -> p b a x u", b=2, a=2, u=2)
-            src = tiles[i][name, b][:].rearrange("p a u x -> p a x u")
-            if name == "v" and (i, b) in V_ON_VECTOR:
-                nc.vector.tensor_copy(out=words[:, b], in_=src)
-            else:
-                nc.scalar.copy(out=words[:, b], in_=src)
+        def unload(i, name, b, dst):
+            words = dst.rearrange("p x j -> p (x j)").bitcast(F32).rearrange("p (a x u) -> p a x u", a=2, u=2)
+            nc.scalar.copy(out=words, in_=tiles[i][name, b][:].rearrange("p a u x -> p a x u"))
 
-        def multiply_de(i, j):
-            t = tiles[i]
-            ps = psum.tile([P, WIN], F32, name="de", bufs=DE_BUFS)
-            t["de", j] = ps
-            cols = slice(P * j, P * (j + 1))
-            nc.tensor.matmul_mx(
-                out=ps[:], lhsT=t["dzt_q"][:, cols], lhsT_scale=t["dzt_s"][:, cols], rhs=t["vt_q"], rhs_scale=t["vt_s"],
-                start=True, stop=True,
-            )
+        def turn_dz(u):
+            turn(u // 2, "dz", u % 2)
+
+        def unload_dz(u):
+            units[u]["dz_t"] = work.tile([P, 2 * P, J], BF16, name="dz_t", align_bytes=64)
+            unload(u // 2, "dz", u % 2, units[u]["dz_t"][:])
+
+        def unload_v(i, b):
+            if b == 0:
+                tiles[i]["v_t"] = work.tile([P, WIN, J], BF16, name="v_t", tag="v_t%d" % (i % 2), bufs=1, align_bytes=64)
+            unload(i, "v", b, tiles[i]["v_t"][:, 2 * P * b : 2 * P * (b + 1), :])
+
+        def multiply_de(u):
+            t = tiles[u // 2]
+            for a in range(2):
+                ps = psum.tile([P, WIN], F32, name="de", bufs=2)
+                units[u]["de", a] = ps
+                cols = slice(P * a, P * (a + 1))
+                nc.tensor.matmul_mx(
+                    out=ps[:], lhsT=units[u]["dz_t", "q"][:, cols], lhsT_scale=units[u]["dz_t", "s"][:, cols], rhs=t["v_t", "q"],
+                    rhs_scale=t["v_t", "s"][:], start=True, stop=True,
+                )
 
         def multiply_dv(i, m):
             t = tiles[i]
-            ps = psum.tile([P, C], F32, name="dv", tag="bank", bufs=BANK_BUFS)
+            ps = psum.tile([P, C], F32, name="dv", tag="bank", bufs=2)
             t["dv", m] = ps
             cols = slice(P * m, P * (m + 1))
             nc.tensor.matmul_mx(
-                out=ps[:], lhsT=t["e_q"][:, cols], lhsT_scale=t["e_s"][:, cols], rhs=t["dz_q"], rhs_scale=t["dz_s"][:],
+                out=ps[:], lhsT=t["e_il", "q"][:, cols], lhsT_scale=t["e_il", "s"][:, cols], rhs=t["dz_il", "q"], rhs_scale=t["dz_il", "s"][:],
                 start=True, stop=True,
             )
 
@@ -229,136 +214,187 @@ def tile_single_head_split_window_attention_1d_v_kernel(
                 dst = image(out_0, r)[x0 : x0 + 2 * P, :].rearrange("(t p) c -> p t c", p=P)
                 nc.sync.dma_start(out=dst, in_=sb[:, m - 1 : m + 1, :])
 
-        def weigh(i, j):
-            if j == 0:
-                tiles[i]["ds"] = work.tile([P, J, WIN], F32, name="ds")
-                tiles[i]["dot"] = small.tile([P, J], F32, name="dot")
-            t = tiles[i]
+        def weigh(u, a):
+            if a == 0:
+                units[u]["dot"] = small.tile([P, 2], F32, name="dot")
+            t = units[u]
             waste = work.tile([P, WIN], F32, name="waste")
             nc.vector.scalar_tensor_tensor(
-                out=waste[:], in0=t["de", j][:], scalar=t["rz"][:, j : j + 1], in1=t["e"][:, j, :], op0=MULT, op1=MULT,
-                accum_out=t["dot"][:, j : j + 1],
+                out=waste[:], in0=t["de", a][:], scalar=t["rz"][:, a : a + 1], in1=tiles[u // 2]["e"][:, 2 * (u % 2) + a, :],
+                op0=MULT, op1=MULT, accum_out=t["dot"][:, a : a + 1],
             )
 
-        def subtract(i, j):
-            n, r = steps[i]
-            t = tiles[i]
-            dst = acc[n] if r == 0 and PE_ROWS[n][j] == 0 else t["ds"]
-            nc.vector.scalar_tensor_tensor(
-                out=dst[:, j, :], in0=t["de", j][:], scalar=t["dot"][:, j : j + 1], in1=t["e"][:, j, :], op0=SUBTRACT, op1=MULT
-            )
+        def subtract(u, a):
+            t = units[u]
+            e = tiles[u // 2]["e"][:, 2 * (u % 2) + a, :]
+            nc.vector.scalar_tensor_tensor(out=e, in0=t["de", a][:], scalar=t["dot"][:, a : a + 1], in1=e, op0=SUBTRACT, op1=MULT)
 
-        def sum_on_tensor(i, j):
+        def sum_rows(i, j):
             n, r = steps[i]
-            if r < PE_ROWS[n][j]:
+            if r < ROWS - 1:
                 if r == 0:
-                    sums[n, j] = psum.tile([P, WIN], F32, name="sum", bufs=SUM_BUFS)
-                nc.tensor.matmul(out=sums[n, j][:], lhsT=ident[:], rhs=tiles[i]["ds"][:, j, :], start=(r == 0), stop=(r == PE_ROWS[n][j] - 1))
-
-        def accumulate(i, j):
-            n, r = steps[i]
-            if PE_ROWS[n][j] == 0 and r > 0:
-                engine = nc.gpsimd if i < G_ACC_UNTIL else nc.vector
-                engine.tensor_tensor(out=acc[n][:, j, :], in0=acc[n][:, j, :], in1=tiles[i]["ds"][:, j, :], op=ADD)
-                if r == ROWS - 1:
-                    store_sum(n, j)
-
-        def store_sum(n, j):
-            nc.sync.dma_start(out=out_1[n].rearrange("(p j) k -> p j k", j=J)[:, j, :], in_=acc[n][:, j, :])
-
-        def empty_sum(i, j):
-            n, r = steps[i]
-            if r == ROWS - 1 and PE_ROWS[n][j] == ROWS:
-                nc.scalar.copy(out=acc[n][:, j, :], in_=sums[n, j][:])
-                store_sum(n, j)
+                    sums[n, j] = psum.tile([P, WIN], F32, name="sum", bufs=J)
+                nc.tensor.matmul(out=sums[n, j][:], lhsT=ident[:], rhs=tiles[i]["e"][:, j, :], start=(r == 0), stop=(r == ROWS - 2))
 
         def merge(i, j):
             n, r = steps[i]
-            if r == ROWS - 1 and PE_ROWS[n][j] == ROWS - 1:
-                nc.vector.tensor_tensor(out=acc[n][:, j, :], in0=sums[n, j][:], in1=tiles[i]["ds"][:, j, :], op=ADD)
-                store_sum(n, j)
+            if r == ROWS - 1:
+                ds = tiles[i]["e"]
+                nc.vector.tensor_tensor(out=ds[:, j, :], in0=sums[n, j][:], in1=ds[:, j, :], op=ADD)
+                nc.sync.dma_start(out=out_1[n].rearrange("(p j) k -> p j k", j=J)[:, j, :], in_=ds[:, j, :])
+
+        pending = []
+
+        def sum_next():
+            if pending:
+                sum_rows(*pending.pop(0))
+
+        def back(u):
+            i, half = divmod(u, 2)
+            weigh(u, 0)
+            weigh(u, 1)
+            unit(u + 2, invert)
+            for a in range(2):
+                subtract(u, a)
+                if steps[i][1] < ROWS - 1:
+                    pending.append((i, 2 * half + a))
+            if 0 <= u - 2 * (ROWS - 1) < J:
+                merge(ROWS - 1, u - 2 * (ROWS - 1))
+
+        def step(i, op, *args):
+            if 0 <= i <= last:
+                op(i, *args)
+
+        def unit(u, op, *args):
+            if u < len(units):
+                op(u, *args)
 
         make_identity(nc, ident[:])
-        nc.vector.memset(warm[:], 0.0)
-        nc.scalar.activation(out=warm[:], in_=warm[:], func=EXP)
         with tc.manual_schedule():
-            for a, b in ((0, 1), (1, 4), (4, 5), (5, 8)):
+            for a, b in ((0, 1), (1, ROWS), (ROWS, 2 * ROWS)):
                 n, r0 = steps[a]
                 src = row_max[r0 : r0 + b - a, n].rearrange("r (p j) -> p r j", j=J)
                 nc.scalar.dma_start(out=rmax[:, a:b, 0:J], in_=src)
-            for a, b in ((0, 1), (1, 8)):
+            nc.vector.memset(warm[:], 0.0)
+            nc.scalar.activation(out=warm[:], in_=warm[:], func=EXP)
+            for a, b in ((0, 1), (1, len(steps))):
                 nc.gpsimd.tensor_scalar(out=neg_max[:, a:b, :], in0=rmax[:, a:b, 0:J], scalar1=-1.0, scalar2=0.0, op0=MULT, op1=ADD)
-            if V_FIRST:
-                load_v(0)
-            load_scores(0, 4)
-            if not V_FIRST:
-                load_v(0)
-            load_grad(0)
-            for i in range(1, 5):
-                load_scores(i, 1)
-                load_grad(i)
-                load_v(i)
+            load_scores(0, 0, 1)
+            load_scores(0, 1, 2)
+            load_grad(0, 0, 2)
+            load_v(0)
+            load_scores(0, 2, J)
+            load_grad(0, 2, J)
+            load_scores(1, 0, 2)
+            load_scores(1, 2, J)
+            load_v(1)
+            load_grad(1, 0, J)
+            load_scores(2, 0, J)
 
-            order = (
-                (sum_on_tensor, -1, 1),
-                (subtract, -1, 3),
-                (sum_on_tensor, -2, 2),
-                (multiply_de, 0, 0),
-                (late_loads, 3),
-                (interleave_e_v, 1),
-                (unload, 1, "v", 0),
-                (multiply_dv, -1, 3),
-                (empty_sum, -2, 0),
-                (accumulate, -2, 3),
-                (interleave_dz, 0),
-                (multiply_de, 0, 1),
-                (empty_sum, -1, 1),
-                (turn, 1, "v", 1),
-                (add_mask_g, 2, 3),
-                (scale, 1),
-                (turn, 1, "dz", 0),
-                (sum_on_tensor, -1, 0),
-                (add_mask, 2),
-                (weigh, 0, 0),
-                (empty_dv, -1, 3),
-                (interleave_e_s, 1),
-                (weigh, 0, 1),
-                (add_mask_g, 2, 2),
-                (add_mask_g, 2, 1),
-                (quantise, 0, "dz", "dz_il", E5M2X4),
-                (turn, 1, "dz", 1),
-                (exponential, 2, 0),
-                (unload, 1, "v", 1),
-                (multiply_dv, 0, 0),
-                (subtract, 0, 0),
-                (unload, 1, "dz", 0),
-                (subtract, 0, 1),
-                (quantise_ev, 1),
-                (exponential, 2, 2),
-                (merge, 0, 0),
-                (unload, 1, "dz", 1),
-                (merge, -1, 2),
-                (multiply_de, 0, 2),
-                (empty_dv, 0, 0),
-                (multiply_dv, 0, 2),
-                (multiply_de, 0, 3),
-                (exponential, 2, 3),
-                (multiply_dv, 0, 1),
-                (merge, 0, 1),
-                (turn, 2, "v", 0),
-                (quantise, 1, "dzt", "dz_t", E5M2X4),
-                (interleave_dz_v, -2),
-                (weigh, 0, 2),
-                (exponential, 2, 1),
-                (empty_sum, -2, 2),
-                (add_mask_g, 2, 0),
-                (empty_dv, 0, 2),
-                (weigh, 0, 3),
-                (empty_dv, 0, 1),
-                (invert, 2),
-                (subtract, 0, 2),
-            )
-            for t in range(-3, last + 4):
-                for op, ahead, *args in order:
-                    if 0 <= t + ahead <= last:
-                        op(t + ahead, *args)
+            for a in range(2):
+                add_mask_vector(0, a, a + 1)
+                exponential(0, a)
+            invert(0)
+            scale(0)
+            turn_dz(0)
+            turn(0, "v", 0)
+            unload_dz(0)
+            turn(0, "v", 1)
+            unload_v(0, 0)
+            unload_v(0, 1)
+            for a in range(2):
+                add_mask_vector(0, 2 + a, 3 + a)
+                exponential(1, a)
+            quantise_dz_t(0)
+            quantise_step(0, "v_t", E4M3X4)
+            multiply_de(0)
+            add_mask_vector(1, 0, 2)
+            invert(1)
+            interleave_e_scalar(0)
+            interleave_e_vector(0)
+            scale(1)
+            quantise_step(0, "e_il", E4M3X4)
+            exponential(2, 0)
+            exponential(2, 1)
+
+            for s in range(last):
+                u = 2 * s
+                step(s + 2, load_v)
+                step(s + 2, load_grad, 0, J)
+                step(s + 3, load_scores, 0, J)
+                unit(u + 3, add_mask_gpsimd, "dz_il%d" % ((s - 1) % 2) if s else "e_il0")
+                turn_dz(u + 1)
+                step(s + 1, turn, "v", 0)
+                unload_dz(u + 1)
+                step(s + 1, turn, "v", 1)
+                step(s + 1, unload_v, 0)
+                interleave_dz(s, 0)
+                step(s - 1, multiply_dv, 0)
+                sum_next()
+                back(u)
+                step(s + 1, unload_v, 1)
+                step(s - 1, multiply_dv, 1)
+                step(s - 1, empty_dv, 0)
+                step(s - 1, multiply_dv, 2)
+
+                quantise_dz_t(u + 1)
+                multiply_de(u + 1)
+                unit(u + 2, scale)
+                if s:
+                    quantise_step(s, "e_il", E4M3X4)
+                step(s + 1, quantise_step, "v_t", E4M3X4)
+                unit(u + 4, add_mask_gpsimd, "v_t%d" % ((s + 1) % 2))
+                unit(u + 3, exponential, 0)
+                step(s - 1, empty_dv, 1)
+                unit(u + 2, turn_dz)
+                sum_next()
+                unit(u + 3, exponential, 1)
+                step(s - 1, empty_dv, 2)
+                step(s + 1, interleave_e_scalar)
+                step(s - 1, multiply_dv, 3)
+                sum_next()
+                unit(u + 2, unload_dz)
+                interleave_dz(s, 1)
+                step(s - 1, empty_dv, 3)
+                back(u + 1)
+
+                unit(u + 2, quantise_dz_t)
+                unit(u + 2, multiply_de)
+                unit(u + 3, scale)
+                step(s + 1, interleave_e_vector)
+                quantise_step(s, "dz_il", E5M2X4)
+                unit(u + 4, exponential, 0)
+                unit(u + 4, exponential, 1)
+
+            s, u = last, 2 * last
+            sum_next()
+            turn_dz(u + 1)
+            multiply_dv(s - 1, 0)
+            sum_next()
+            interleave_dz(s, 0)
+            interleave_dz(s, 1)
+            unload_dz(u + 1)
+            multiply_dv(s - 1, 1)
+            back(u)
+            for m in range(J):
+                empty_dv(s - 1, m)
+                if m + 2 < J:
+                    multiply_dv(s - 1, m + 2)
+                if m == 0:
+                    sum_next()
+            quantise_dz_t(u + 1)
+            multiply_de(u + 1)
+            quantise_step(s, "e_il", E4M3X4)
+            quantise_step(s, "dz_il", E5M2X4)
+            multiply_dv(s, 0)
+            multiply_dv(s, 1)
+            sum_next()
+            merge(s, 0)
+            merge(s, 1)
+            for m in range(J):
+                empty_dv(s, m)
+                if m + 2 < J:
+                    multiply_dv(s, m + 2)
+            back(u + 1)
+            merge(s, 2)
+            merge(s, 3)

@@ -20,7 +20,7 @@ WIN = 512
 C = 512
 ROWS = 4
 SPLITS = 2
-E_ON_SCALAR = 64
+DZ_ON_SCALAR = 512
 
 FLOPS = 2 * ROWS * SPLITS * 2 * WIN * WIN * C
 BYTES = 4 * ROWS * SPLITS * WIN * WIN + 2 * 2 * (ROWS * SPLITS * WIN * C) + 2 * SPLITS * WIN * WIN + 4 * ROWS * SPLITS * WIN * C + 4 * SPLITS * WIN * WIN
@@ -59,6 +59,11 @@ def tile_single_head_split_window_attention_1d_v_kernel(
                 return [(0, first + start, WIN)]
             head = w - start
             return [(0, first + start, head), (head, first, WIN - head)]
+
+        def load_row_max(a, b, queue):
+            n, r0 = steps[a]
+            queue.dma_start(out=rmax[:, a:b, 0:J], in_=row_max[r0 : r0 + b - a, n].rearrange("r (p j) -> p r j", j=J))
+            nc.gpsimd.tensor_scalar(out=neg_max[:, a:b, :], in0=rmax[:, a:b, 0:J], scalar1=-1.0, scalar2=0.0, op0=MULT, op1=ADD)
 
         def load_scores(i, a, b):
             n, r = steps[i]
@@ -122,7 +127,8 @@ def tile_single_head_split_window_attention_1d_v_kernel(
             for a in range(2):
                 j = 2 * half + a
                 nc.vector.tensor_scalar(
-                    out=tiles[i]["dz"][:, j, :], in0=tiles[i]["g"][:, j, :], scalar1=units[u]["rz"][:, a : a + 1], scalar2=None, op0=MULT
+                    out=tiles[i]["dz"][:, j, :].rearrange("p (u x e) -> p u x e", u=2, e=2),
+                    in0=tiles[i]["g"][:, j, :].rearrange("p (x u e) -> p u x e", u=2, e=2), scalar1=units[u]["rz"][:, a : a + 1], scalar2=None, op0=MULT
                 )
 
         def four_by_four(dst, src, cols):
@@ -131,17 +137,19 @@ def tile_single_head_split_window_attention_1d_v_kernel(
                 in_=src[:, :, cols].rearrange("p j (c i) -> p c j i", i=4),
             )
 
-        def interleave_e_scalar(i):
+        def interleave_e(i):
             tiles[i]["e_il"] = work.tile([P, WIN, J], BF16, name="e_il", tag="e_il%d" % (i % 2), bufs=1, align_bytes=64)
-            nc.scalar.copy(**four_by_four(tiles[i]["e_il"], tiles[i]["e"], slice(0, E_ON_SCALAR)))
+            nc.vector.tensor_copy(**four_by_four(tiles[i]["e_il"], tiles[i]["e"], slice(0, WIN)))
 
-        def interleave_e_vector(i):
-            nc.vector.tensor_copy(**four_by_four(tiles[i]["e_il"], tiles[i]["e"], slice(E_ON_SCALAR, WIN)))
-
-        def interleave_dz(i, half):
-            if half == 0:
+        def interleave_dz(i, part):
+            if part == 0:
                 tiles[i]["dz_il"] = work.tile([P, C, J], BF16, name="dz_il", tag="dz_il%d" % (i % 2), bufs=1, align_bytes=64)
-            nc.scalar.copy(**four_by_four(tiles[i]["dz_il"], tiles[i]["dz"], slice(half * C // 2, (half + 1) * C // 2)))
+            width = DZ_ON_SCALAR // 4
+            nc.scalar.copy(**four_by_four(tiles[i]["dz_il"], tiles[i]["dz"], slice(part * width, (part + 1) * width)))
+
+        def interleave_dz_rest(i):
+            if DZ_ON_SCALAR < C:
+                nc.vector.tensor_copy(**four_by_four(tiles[i]["dz_il"], tiles[i]["dz"], slice(DZ_ON_SCALAR, C)))
 
         def quantise(held, name, fmt):
             src = held[name][:].rearrange("p a b -> p (a b)")
@@ -164,7 +172,8 @@ def tile_single_head_split_window_attention_1d_v_kernel(
             tiles[i][name, b] = ps
             for a in range(2):
                 for u in range(2):
-                    nc.tensor.transpose(ps[:, a, u, :], words[:, 2 * b + a, u : C // 2 : 2], ident[:])
+                    picked = slice(u, C // 2, 2) if name == "v" else slice(u * P, (u + 1) * P)
+                    nc.tensor.transpose(ps[:, a, u, :], words[:, 2 * b + a, picked], ident[:])
 
         def unload(i, name, b, dst):
             words = dst.rearrange("p x j -> p (x j)").bitcast(F32).rearrange("p (a x u) -> p a x u", a=2, u=2)
@@ -208,7 +217,10 @@ def tile_single_head_split_window_attention_1d_v_kernel(
             if m == 0:
                 tiles[i]["dv_sb"] = work.tile([P, J, C], F32, name="dv_sb")
             sb = tiles[i]["dv_sb"]
-            nc.scalar.copy(out=sb[:, m, :], in_=tiles[i]["dv", m][:])
+            nc.scalar.copy(
+                out=sb[:, m, :].rearrange("p (x u e) -> p x u e", u=2, e=2),
+                in_=tiles[i]["dv", m][:].rearrange("p (u x e) -> p x u e", u=2, e=2),
+            )
             if m % 2:
                 x0 = [x0 + P * (m - 1) - win0 for win0, x0, rows in spans(n, r) if win0 <= P * (m - 1) < win0 + rows][0]
                 dst = image(out_0, r)[x0 : x0 + 2 * P, :].rearrange("(t p) c -> p t c", p=P)
@@ -258,8 +270,8 @@ def tile_single_head_split_window_attention_1d_v_kernel(
                 subtract(u, a)
                 if steps[i][1] < ROWS - 1:
                     pending.append((i, 2 * half + a))
-            if 0 <= u - 2 * (ROWS - 1) < J:
-                merge(ROWS - 1, u - 2 * (ROWS - 1))
+            if 0 <= u - (2 * ROWS - 1) < J:
+                merge(ROWS - 1, u - (2 * ROWS - 1))
 
         def step(i, op, *args):
             if 0 <= i <= last:
@@ -271,49 +283,43 @@ def tile_single_head_split_window_attention_1d_v_kernel(
 
         make_identity(nc, ident[:])
         with tc.manual_schedule():
-            for a, b in ((0, 1), (1, ROWS), (ROWS, 2 * ROWS)):
-                n, r0 = steps[a]
-                src = row_max[r0 : r0 + b - a, n].rearrange("r (p j) -> p r j", j=J)
-                nc.scalar.dma_start(out=rmax[:, a:b, 0:J], in_=src)
+            load_row_max(0, 1, nc.scalar)
             nc.vector.memset(warm[:], 0.0)
             nc.scalar.activation(out=warm[:], in_=warm[:], func=EXP)
-            for a, b in ((0, 1), (1, len(steps))):
-                nc.gpsimd.tensor_scalar(out=neg_max[:, a:b, :], in0=rmax[:, a:b, 0:J], scalar1=-1.0, scalar2=0.0, op0=MULT, op1=ADD)
-            load_scores(0, 0, 1)
-            load_scores(0, 1, 2)
+            for j in range(J):
+                load_scores(0, j, j + 1)
             load_grad(0, 0, 2)
             load_v(0)
-            load_scores(0, 2, J)
             load_grad(0, 2, J)
+            load_row_max(1, ROWS, nc.sync)
+            load_row_max(ROWS, 2 * ROWS, nc.sync)
             load_scores(1, 0, 2)
             load_scores(1, 2, J)
             load_v(1)
             load_grad(1, 0, J)
             load_scores(2, 0, J)
 
-            for a in range(2):
-                add_mask_vector(0, a, a + 1)
-                exponential(0, a)
+            for j in range(J):
+                add_mask_vector(0, j, j + 1)
+                exponential(j // 2, j % 2)
             invert(0)
             scale(0)
             turn_dz(0)
             turn(0, "v", 0)
+            invert(1)
+            interleave_e(0)
             unload_dz(0)
             turn(0, "v", 1)
             unload_v(0, 0)
             unload_v(0, 1)
-            for a in range(2):
-                add_mask_vector(0, 2 + a, 3 + a)
-                exponential(1, a)
+            scale(1)
             quantise_dz_t(0)
+            add_mask_vector(1, 0, 2)
             quantise_step(0, "v_t", E4M3X4)
             multiply_de(0)
-            add_mask_vector(1, 0, 2)
-            invert(1)
-            interleave_e_scalar(0)
-            interleave_e_vector(0)
-            scale(1)
             quantise_step(0, "e_il", E4M3X4)
+            turn_dz(1)
+            turn(1, "v", 0)
             exponential(2, 0)
             exponential(2, 1)
 
@@ -323,72 +329,82 @@ def tile_single_head_split_window_attention_1d_v_kernel(
                 step(s + 2, load_grad, 0, J)
                 step(s + 3, load_scores, 0, J)
                 unit(u + 3, add_mask_gpsimd, "dz_il%d" % ((s - 1) % 2) if s else "e_il0")
-                turn_dz(u + 1)
-                step(s + 1, turn, "v", 0)
-                unload_dz(u + 1)
-                step(s + 1, turn, "v", 1)
-                step(s + 1, unload_v, 0)
-                interleave_dz(s, 0)
+                sum_next()
                 step(s - 1, multiply_dv, 0)
+                interleave_dz(s, 0)
+                unload_dz(u + 1)
+                step(s - 1, multiply_dv, 1)
+                if s == 0:
+                    turn(1, "v", 1)
+                    unload_v(1, 0)
+                    unload_v(1, 1)
                 sum_next()
                 back(u)
-                step(s + 1, unload_v, 1)
-                step(s - 1, multiply_dv, 1)
+                interleave_dz(s, 1)
                 step(s - 1, empty_dv, 0)
-                step(s - 1, multiply_dv, 2)
 
                 quantise_dz_t(u + 1)
                 multiply_de(u + 1)
-                unit(u + 2, scale)
+                step(s - 1, multiply_dv, 2)
+                scale(u + 2)
                 if s:
                     quantise_step(s, "e_il", E4M3X4)
-                step(s + 1, quantise_step, "v_t", E4M3X4)
+                quantise_step(s + 1, "v_t", E4M3X4)
                 unit(u + 4, add_mask_gpsimd, "v_t%d" % ((s + 1) % 2))
-                unit(u + 3, exponential, 0)
+                exponential(u + 3, 0)
                 step(s - 1, empty_dv, 1)
-                unit(u + 2, turn_dz)
+                turn_dz(u + 2)
                 sum_next()
-                unit(u + 3, exponential, 1)
+                exponential(u + 3, 1)
                 step(s - 1, empty_dv, 2)
-                step(s + 1, interleave_e_scalar)
                 step(s - 1, multiply_dv, 3)
-                sum_next()
-                unit(u + 2, unload_dz)
-                interleave_dz(s, 1)
+                interleave_dz(s, 2)
+                unload_dz(u + 2)
+                step(s + 2, turn, "v", 0)
+                if s == last - 1:
+                    sum_next()
+                interleave_dz(s, 3)
                 step(s - 1, empty_dv, 3)
                 back(u + 1)
 
-                unit(u + 2, quantise_dz_t)
-                unit(u + 2, multiply_de)
-                unit(u + 3, scale)
-                step(s + 1, interleave_e_vector)
+                quantise_dz_t(u + 2)
+                multiply_de(u + 2)
+                step(s + 2, turn, "v", 1)
+                scale(u + 3)
+                interleave_dz_rest(s)
+                interleave_e(s + 1)
                 quantise_step(s, "dz_il", E5M2X4)
                 unit(u + 4, exponential, 0)
+                step(s + 2, unload_v, 0)
+                turn_dz(u + 3)
                 unit(u + 4, exponential, 1)
+                step(s + 2, unload_v, 1)
 
             s, u = last, 2 * last
             sum_next()
-            turn_dz(u + 1)
-            multiply_dv(s - 1, 0)
             sum_next()
-            interleave_dz(s, 0)
-            interleave_dz(s, 1)
+            multiply_dv(s - 1, 0)
+            for part in range(3):
+                interleave_dz(s, part)
             unload_dz(u + 1)
+            interleave_dz(s, 3)
             multiply_dv(s - 1, 1)
+            sum_next()
             back(u)
-            for m in range(J):
-                empty_dv(s - 1, m)
-                if m + 2 < J:
-                    multiply_dv(s - 1, m + 2)
-                if m == 0:
-                    sum_next()
+            empty_dv(s - 1, 0)
+            multiply_dv(s - 1, 2)
+            empty_dv(s - 1, 1)
             quantise_dz_t(u + 1)
+            multiply_dv(s - 1, 3)
             multiply_de(u + 1)
+            sum_next()
+            interleave_dz_rest(s)
             quantise_step(s, "e_il", E4M3X4)
             quantise_step(s, "dz_il", E5M2X4)
+            empty_dv(s - 1, 2)
+            empty_dv(s - 1, 3)
             multiply_dv(s, 0)
             multiply_dv(s, 1)
-            sum_next()
             merge(s, 0)
             merge(s, 1)
             for m in range(J):

@@ -20,7 +20,6 @@ WIN = 512
 C = 512
 ROWS = 4
 SPLITS = 2
-DZ_ON_SCALAR = 512
 
 FLOPS = 2 * ROWS * SPLITS * 2 * WIN * WIN * C
 BYTES = 4 * ROWS * SPLITS * WIN * WIN + 2 * 2 * (ROWS * SPLITS * WIN * C) + 2 * SPLITS * WIN * WIN + 4 * ROWS * SPLITS * WIN * C + 4 * SPLITS * WIN * WIN
@@ -144,12 +143,15 @@ def tile_single_head_split_window_attention_1d_v_kernel(
         def interleave_dz(i, part):
             if part == 0:
                 tiles[i]["dz_il"] = work.tile([P, C, J], BF16, name="dz_il", tag="dz_il%d" % (i % 2), bufs=1, align_bytes=64)
-            width = DZ_ON_SCALAR // 4
-            nc.scalar.copy(**four_by_four(tiles[i]["dz_il"], tiles[i]["dz"], slice(part * width, (part + 1) * width)))
+            if part < scalar_parts(i):
+                nc.scalar.copy(**four_by_four(tiles[i]["dz_il"], tiles[i]["dz"], slice(part * P, (part + 1) * P)))
+
+        def scalar_parts(i):
+            return {0: 3, ROWS + 1: 3, last: 2}.get(i, 4)
 
         def interleave_dz_rest(i):
-            if DZ_ON_SCALAR < C:
-                nc.vector.tensor_copy(**four_by_four(tiles[i]["dz_il"], tiles[i]["dz"], slice(DZ_ON_SCALAR, C)))
+            if scalar_parts(i) < 4:
+                nc.vector.tensor_copy(**four_by_four(tiles[i]["dz_il"], tiles[i]["dz"], slice(scalar_parts(i) * P, C)))
 
         def quantise(held, name, fmt):
             src = held[name][:].rearrange("p a b -> p (a b)")
@@ -194,7 +196,10 @@ def tile_single_head_split_window_attention_1d_v_kernel(
         def multiply_de(u):
             t = tiles[u // 2]
             for a in range(2):
-                ps = psum.tile([P, WIN], F32, name="de", bufs=2)
+                if u < len(units) - 1:
+                    ps = psum.tile([P, WIN], F32, name="de", bufs=2)
+                else:
+                    ps = psum.tile([P, WIN], F32, name="de_last", tag="sum", bufs=J)
                 units[u]["de", a] = ps
                 cols = slice(P * a, P * (a + 1))
                 nc.tensor.matmul_mx(
@@ -241,25 +246,39 @@ def tile_single_head_split_window_attention_1d_v_kernel(
             e = tiles[u // 2]["e"][:, 2 * (u % 2) + a, :]
             nc.vector.scalar_tensor_tensor(out=e, in0=t["de", a][:], scalar=t["dot"][:, a : a + 1], in1=e, op0=SUBTRACT, op1=MULT)
 
-        def sum_rows(i, j):
-            n, r = steps[i]
-            if r < ROWS - 1:
-                if r == 0:
-                    sums[n, j] = psum.tile([P, WIN], F32, name="sum", bufs=J)
-                nc.tensor.matmul(out=sums[n, j][:], lhsT=ident[:], rhs=tiles[i]["e"][:, j, :], start=(r == 0), stop=(r == ROWS - 2))
-
-        def merge(i, j):
-            n, r = steps[i]
-            if r == ROWS - 1:
-                ds = tiles[i]["e"]
-                nc.vector.tensor_tensor(out=ds[:, j, :], in0=sums[n, j][:], in1=ds[:, j, :], op=ADD)
-                nc.sync.dma_start(out=out_1[n].rearrange("(p j) k -> p j k", j=J)[:, j, :], in_=ds[:, j, :])
-
-        pending = []
+        def store_sum(n, j, src):
+            nc.sync.dma_start(out=out_1[n].rearrange("(p j) k -> p j k", j=J)[:, j, :], in_=src)
 
         def sum_next():
             if pending:
-                sum_rows(*pending.pop(0))
+                i, j = pending.pop(0)
+                n, r = steps[i]
+                if r == 0:
+                    sums[n, j] = psum.tile([P, WIN], F32, name="sum", bufs=J)
+                nc.tensor.matmul(out=sums[n, j][:], lhsT=ident[:], rhs=tiles[i]["e"][:, j, :], start=(r == 0), stop=(r == ROWS - 1 - n))
+
+        def empty_sum(j):
+            ds = tiles[ROWS - 1]["e"]
+            nc.scalar.copy(out=ds[:, j, :], in_=sums[0, j][:])
+            store_sum(0, j, ds[:, j, :])
+
+        def merge(j):
+            ds = tiles[last]["e"]
+            nc.vector.tensor_tensor(out=ds[:, j, :], in0=sums[1, j][:], in1=ds[:, j, :], op=ADD)
+            store_sum(1, j, ds[:, j, :])
+
+        def add_row_gpsimd(i, tag):
+            total = work.tile([P, 2, WIN], F32, name="total", tag=tag, bufs=1, align_bytes=64)
+            before = sums.get("gpsimd", tiles[ROWS]["e"])
+            if i < last:
+                nc.gpsimd.tensor_tensor(out=total[:], in0=before[:, 0:2, :], in1=tiles[i]["e"][:, 0:2, :], op=ADD)
+            else:
+                for j in range(2):
+                    nc.gpsimd.tensor_tensor(out=total[:, j, :], in0=before[:, j, :], in1=tiles[i]["e"][:, j, :], op=ADD)
+                    store_sum(1, j, total[:, j, :])
+            sums["gpsimd"] = total
+
+        pending = []
 
         def back(u):
             i, half = divmod(u, 2)
@@ -268,10 +287,8 @@ def tile_single_head_split_window_attention_1d_v_kernel(
             unit(u + 2, invert)
             for a in range(2):
                 subtract(u, a)
-                if steps[i][1] < ROWS - 1:
+                if i < ROWS or (half == 1 and i < last):
                     pending.append((i, 2 * half + a))
-            if 0 <= u - (2 * ROWS - 1) < J:
-                merge(ROWS - 1, u - (2 * ROWS - 1))
 
         def step(i, op, *args):
             if 0 <= i <= last:
@@ -294,8 +311,8 @@ def tile_single_head_split_window_attention_1d_v_kernel(
             load_row_max(1, ROWS, nc.sync)
             load_row_max(ROWS, 2 * ROWS, nc.sync)
             load_scores(1, 0, 2)
-            load_scores(1, 2, J)
             load_v(1)
+            load_scores(1, 2, J)
             load_grad(1, 0, J)
             load_scores(2, 0, J)
 
@@ -313,13 +330,13 @@ def tile_single_head_split_window_attention_1d_v_kernel(
             unload_v(0, 0)
             unload_v(0, 1)
             scale(1)
+            turn_dz(1)
             quantise_dz_t(0)
             add_mask_vector(1, 0, 2)
+            turn(1, "v", 0)
             quantise_step(0, "v_t", E4M3X4)
             multiply_de(0)
             quantise_step(0, "e_il", E4M3X4)
-            turn_dz(1)
-            turn(1, "v", 0)
             exponential(2, 0)
             exponential(2, 1)
 
@@ -328,7 +345,7 @@ def tile_single_head_split_window_attention_1d_v_kernel(
                 step(s + 2, load_v)
                 step(s + 2, load_grad, 0, J)
                 step(s + 3, load_scores, 0, J)
-                unit(u + 3, add_mask_gpsimd, "dz_il%d" % ((s - 1) % 2) if s else "e_il0")
+                unit(u + 3, add_mask_gpsimd, "dz_il%d" % ((s - 1) % 2) if s else "v_t0")
                 sum_next()
                 step(s - 1, multiply_dv, 0)
                 interleave_dz(s, 0)
@@ -342,15 +359,21 @@ def tile_single_head_split_window_attention_1d_v_kernel(
                 back(u)
                 interleave_dz(s, 1)
                 step(s - 1, empty_dv, 0)
+                if s == ROWS + 1:
+                    empty_sum(0)
 
                 quantise_dz_t(u + 1)
                 multiply_de(u + 1)
                 step(s - 1, multiply_dv, 2)
                 scale(u + 2)
+                quantise_step(s + 1, "v_t", E4M3X4)
                 if s:
                     quantise_step(s, "e_il", E4M3X4)
-                quantise_step(s + 1, "v_t", E4M3X4)
+                else:
+                    interleave_dz_rest(s)
                 unit(u + 4, add_mask_gpsimd, "v_t%d" % ((s + 1) % 2))
+                if s == last - 1:
+                    add_row_gpsimd(s - 1, "v_t%d" % ((s + 1) % 2))
                 exponential(u + 3, 0)
                 step(s - 1, empty_dv, 1)
                 turn_dz(u + 2)
@@ -365,15 +388,18 @@ def tile_single_head_split_window_attention_1d_v_kernel(
                     sum_next()
                 interleave_dz(s, 3)
                 step(s - 1, empty_dv, 3)
+                if s == ROWS + 1:
+                    empty_sum(1)
                 back(u + 1)
 
                 quantise_dz_t(u + 2)
                 multiply_de(u + 2)
                 step(s + 2, turn, "v", 1)
+                if s:
+                    interleave_dz_rest(s)
                 scale(u + 3)
-                interleave_dz_rest(s)
-                interleave_e(s + 1)
                 quantise_step(s, "dz_il", E5M2X4)
+                interleave_e(s + 1)
                 unit(u + 4, exponential, 0)
                 step(s + 2, unload_v, 0)
                 turn_dz(u + 3)
@@ -381,36 +407,37 @@ def tile_single_head_split_window_attention_1d_v_kernel(
                 step(s + 2, unload_v, 1)
 
             s, u = last, 2 * last
-            sum_next()
-            sum_next()
             multiply_dv(s - 1, 0)
-            for part in range(3):
-                interleave_dz(s, part)
+            sum_next()
+            interleave_dz(s, 0)
+            interleave_dz(s, 1)
             unload_dz(u + 1)
-            interleave_dz(s, 3)
             multiply_dv(s - 1, 1)
             sum_next()
-            back(u)
+            empty_sum(2)
+            empty_sum(3)
+            interleave_dz_rest(s)
+            quantise_dz_t(u + 1)
+            quantise_step(s, "e_il", E4M3X4)
+            quantise_step(s, "dz_il", E5M2X4)
+            add_row_gpsimd(s - 1, "e_il%d" % (s % 2))
             empty_dv(s - 1, 0)
             multiply_dv(s - 1, 2)
             empty_dv(s - 1, 1)
-            quantise_dz_t(u + 1)
             multiply_dv(s - 1, 3)
             multiply_de(u + 1)
-            sum_next()
-            interleave_dz_rest(s)
-            quantise_step(s, "e_il", E4M3X4)
-            quantise_step(s, "dz_il", E5M2X4)
             empty_dv(s - 1, 2)
-            empty_dv(s - 1, 3)
             multiply_dv(s, 0)
+            empty_dv(s - 1, 3)
             multiply_dv(s, 1)
-            merge(s, 0)
-            merge(s, 1)
-            for m in range(J):
-                empty_dv(s, m)
-                if m + 2 < J:
-                    multiply_dv(s, m + 2)
+            back(u)
+            empty_dv(s, 0)
+            multiply_dv(s, 2)
+            empty_dv(s, 1)
+            multiply_dv(s, 3)
+            empty_dv(s, 2)
+            empty_dv(s, 3)
+            add_row_gpsimd(s, "dz_il%d" % ((s - 1) % 2))
             back(u + 1)
-            merge(s, 2)
-            merge(s, 3)
+            merge(2)
+            merge(3)

@@ -62,7 +62,9 @@ def tile_single_head_split_window_attention_1d_v_kernel(
         def load_row_max(a, b, queue):
             n, r0 = steps[a]
             queue.dma_start(out=rmax[:, a:b, 0:J], in_=row_max[r0 : r0 + b - a, n].rearrange("r (p j) -> p r j", j=J))
-            nc.gpsimd.tensor_scalar(out=neg_max[:, a:b, :], in0=rmax[:, a:b, 0:J], scalar1=-1.0, scalar2=0.0, op0=MULT, op1=ADD)
+
+        def negate_row_max(a, b, engine):
+            engine.tensor_scalar(out=neg_max[:, a:b, :], in0=rmax[:, a:b, 0:J], scalar1=-1.0, scalar2=0.0, op0=MULT, op1=ADD)
 
         def load_scores(i, a, b):
             n, r = steps[i]
@@ -130,15 +132,15 @@ def tile_single_head_split_window_attention_1d_v_kernel(
                     in0=tiles[i]["g"][:, j, :].rearrange("p (x u e) -> p u x e", u=2, e=2), scalar1=units[u]["rz"][:, a : a + 1], scalar2=None, op0=MULT
                 )
 
-        def four_by_four(dst, src, cols):
+        def four_by_four(dst, src, cols, run=4):
             return dict(
-                out=dst[:, cols, :].rearrange("p (c i) j -> p c j i", i=4),
-                in_=src[:, :, cols].rearrange("p j (c i) -> p c j i", i=4),
+                out=dst[:, cols, :].rearrange("p (c i) j -> p c j i", i=run),
+                in_=src[:, :, cols].rearrange("p j (c i) -> p c j i", i=run),
             )
 
         def interleave_e(i):
             tiles[i]["e_il"] = work.tile([P, WIN, J], BF16, name="e_il", tag="e_il%d" % (i % 2), bufs=1, align_bytes=64)
-            nc.vector.tensor_copy(**four_by_four(tiles[i]["e_il"], tiles[i]["e"], slice(0, WIN)))
+            nc.vector.tensor_copy(**four_by_four(tiles[i]["e_il"], tiles[i]["e"], slice(0, WIN), 2))
 
         def interleave_dz(i, part):
             if part == 0:
@@ -209,7 +211,7 @@ def tile_single_head_split_window_attention_1d_v_kernel(
 
         def multiply_dv(i, m):
             t = tiles[i]
-            ps = psum.tile([P, C], F32, name="dv", tag="bank", bufs=2)
+            ps = psum.tile([P, C], F32, name="dv", tag="de" if i == last and m >= 2 else "bank", bufs=2)
             t["dv", m] = ps
             cols = slice(P * m, P * (m + 1))
             nc.tensor.matmul_mx(
@@ -226,10 +228,12 @@ def tile_single_head_split_window_attention_1d_v_kernel(
                 out=sb[:, m, :].rearrange("p (x u e) -> p x u e", u=2, e=2),
                 in_=tiles[i]["dv", m][:].rearrange("p (u x e) -> p x u e", u=2, e=2),
             )
-            if m % 2:
-                x0 = [x0 + P * (m - 1) - win0 for win0, x0, rows in spans(n, r) if win0 <= P * (m - 1) < win0 + rows][0]
-                dst = image(out_0, r)[x0 : x0 + 2 * P, :].rearrange("(t p) c -> p t c", p=P)
-                nc.sync.dma_start(out=dst, in_=sb[:, m - 1 : m + 1, :])
+            count = 1 if i == last else 2
+            if (m + 1) % count == 0:
+                m0 = m + 1 - count
+                x0 = [x0 + P * m0 - win0 for win0, x0, rows in spans(n, r) if win0 <= P * m0 < win0 + rows][0]
+                dst = image(out_0, r)[x0 : x0 + count * P, :].rearrange("(t p) c -> p t c", p=P)
+                nc.sync.dma_start(out=dst, in_=sb[:, m0 : m + 1, :])
 
         def weigh(u, a):
             if a == 0:
@@ -249,13 +253,17 @@ def tile_single_head_split_window_attention_1d_v_kernel(
         def store_sum(n, j, src):
             nc.sync.dma_start(out=out_1[n].rearrange("(p j) k -> p j k", j=J)[:, j, :], in_=src)
 
-        def sum_next():
-            if pending:
-                i, j = pending.pop(0)
+        def sum_next(count=1):
+            for i, j, half in pending[:count]:
                 n, r = steps[i]
-                if r == 0:
+                if r == 0 and half == 0:
                     sums[n, j] = psum.tile([P, WIN], F32, name="sum", bufs=J)
-                nc.tensor.matmul(out=sums[n, j][:], lhsT=ident[:], rhs=tiles[i]["e"][:, j, :], start=(r == 0), stop=(r == ROWS - 1 - n))
+                cols = slice(half * WIN // 2, (half + 1) * WIN // 2)
+                nc.tensor.matmul(
+                    out=sums[n, j][:, cols], lhsT=ident[:], rhs=tiles[i]["e"][:, j, cols],
+                    start=(r == 0 and half == 0), stop=(r == ROWS - 1 - n and half == 1),
+                )
+            pending[:count] = []
 
         def empty_sum(j):
             ds = tiles[ROWS - 1]["e"]
@@ -288,7 +296,7 @@ def tile_single_head_split_window_attention_1d_v_kernel(
             for a in range(2):
                 subtract(u, a)
                 if i < ROWS or (half == 1 and i < last):
-                    pending.append((i, 2 * half + a))
+                    pending.extend((i, 2 * half + a, b) for b in range(2))
 
         def step(i, op, *args):
             if 0 <= i <= last:
@@ -301,43 +309,49 @@ def tile_single_head_split_window_attention_1d_v_kernel(
         make_identity(nc, ident[:])
         with tc.manual_schedule():
             load_row_max(0, 1, nc.scalar)
+            negate_row_max(0, 1, nc.gpsimd)
             nc.vector.memset(warm[:], 0.0)
             nc.scalar.activation(out=warm[:], in_=warm[:], func=EXP)
             for j in range(J):
                 load_scores(0, j, j + 1)
-            load_grad(0, 0, 2)
             load_v(0)
+            load_grad(0, 0, 2)
             load_grad(0, 2, J)
-            load_row_max(1, ROWS, nc.sync)
-            load_row_max(ROWS, 2 * ROWS, nc.sync)
+            load_row_max(1, 2, nc.sync)
             load_scores(1, 0, 2)
             load_v(1)
             load_scores(1, 2, J)
             load_grad(1, 0, J)
             load_scores(2, 0, J)
+            load_row_max(2, ROWS, nc.sync)
+            load_row_max(ROWS, 2 * ROWS, nc.sync)
 
             for j in range(J):
                 add_mask_vector(0, j, j + 1)
                 exponential(j // 2, j % 2)
-            invert(0)
-            scale(0)
-            turn_dz(0)
             turn(0, "v", 0)
-            invert(1)
-            interleave_e(0)
-            unload_dz(0)
             turn(0, "v", 1)
+            invert(0)
+            invert(1)
+            scale(0)
             unload_v(0, 0)
+            turn_dz(0)
             unload_v(0, 1)
+            interleave_e(0)
             scale(1)
             turn_dz(1)
-            quantise_dz_t(0)
-            add_mask_vector(1, 0, 2)
-            turn(1, "v", 0)
+            unload_dz(0)
+            negate_row_max(1, 2, nc.vector)
+            add_mask_vector(1, 0, 1)
             quantise_step(0, "v_t", E4M3X4)
+            quantise_dz_t(0)
             multiply_de(0)
-            quantise_step(0, "e_il", E4M3X4)
             exponential(2, 0)
+            unload_dz(1)
+            turn(1, "v", 0)
+            turn(1, "v", 1)
+            quantise_step(0, "e_il", E4M3X4)
+            add_mask_vector(1, 1, 2)
             exponential(2, 1)
 
             for s in range(last):
@@ -345,19 +359,20 @@ def tile_single_head_split_window_attention_1d_v_kernel(
                 step(s + 2, load_v)
                 step(s + 2, load_grad, 0, J)
                 step(s + 3, load_scores, 0, J)
-                unit(u + 3, add_mask_gpsimd, "dz_il%d" % ((s - 1) % 2) if s else "v_t0")
+                unit(u + 3, add_mask_gpsimd, "dz_il%d" % ((s - 1) % 2) if s else "e_il0")
                 sum_next()
-                step(s - 1, multiply_dv, 0)
                 interleave_dz(s, 0)
-                unload_dz(u + 1)
-                step(s - 1, multiply_dv, 1)
-                if s == 0:
-                    turn(1, "v", 1)
-                    unload_v(1, 0)
+                unload_v(s + 1, 1 if s else 0)
+                step(s - 1, multiply_dv, 0)
+                sum_next()
+                interleave_dz(s, 1)
+                if s:
+                    unload_dz(u + 1)
+                else:
                     unload_v(1, 1)
+                step(s - 1, multiply_dv, 1)
                 sum_next()
                 back(u)
-                interleave_dz(s, 1)
                 step(s - 1, empty_dv, 0)
                 if s == ROWS + 1:
                     empty_sum(0)
@@ -377,23 +392,28 @@ def tile_single_head_split_window_attention_1d_v_kernel(
                 exponential(u + 3, 0)
                 step(s - 1, empty_dv, 1)
                 turn_dz(u + 2)
-                sum_next()
+                sum_next(2)
                 exponential(u + 3, 1)
                 step(s - 1, empty_dv, 2)
-                step(s - 1, multiply_dv, 3)
+                step(s + 2, turn, "v", 0)
                 interleave_dz(s, 2)
                 unload_dz(u + 2)
-                step(s + 2, turn, "v", 0)
+                step(s - 1, multiply_dv, 3)
                 if s == last - 1:
-                    sum_next()
+                    sum_next(2)
                 interleave_dz(s, 3)
-                step(s - 1, empty_dv, 3)
+                step(s + 2, unload_v, 0)
+                if s == ROWS + 2:
+                    empty_sum(2)
                 if s == ROWS + 1:
                     empty_sum(1)
                 back(u + 1)
 
+                if s == 0:
+                    negate_row_max(2, len(steps), nc.vector)
                 quantise_dz_t(u + 2)
                 multiply_de(u + 2)
+                sum_next()
                 step(s + 2, turn, "v", 1)
                 if s:
                     interleave_dz_rest(s)
@@ -401,21 +421,18 @@ def tile_single_head_split_window_attention_1d_v_kernel(
                 quantise_step(s, "dz_il", E5M2X4)
                 interleave_e(s + 1)
                 unit(u + 4, exponential, 0)
-                step(s + 2, unload_v, 0)
+                step(s - 1, empty_dv, 3)
                 turn_dz(u + 3)
                 unit(u + 4, exponential, 1)
-                step(s + 2, unload_v, 1)
 
             s, u = last, 2 * last
             multiply_dv(s - 1, 0)
             sum_next()
-            interleave_dz(s, 0)
-            interleave_dz(s, 1)
-            unload_dz(u + 1)
-            multiply_dv(s - 1, 1)
-            sum_next()
-            empty_sum(2)
             empty_sum(3)
+            interleave_dz(s, 0)
+            unload_dz(u + 1)
+            interleave_dz(s, 1)
+            multiply_dv(s - 1, 1)
             interleave_dz_rest(s)
             quantise_dz_t(u + 1)
             quantise_step(s, "e_il", E4M3X4)
@@ -425,18 +442,18 @@ def tile_single_head_split_window_attention_1d_v_kernel(
             multiply_dv(s - 1, 2)
             empty_dv(s - 1, 1)
             multiply_dv(s - 1, 3)
-            multiply_de(u + 1)
+            sum_next()
             empty_dv(s - 1, 2)
             multiply_dv(s, 0)
             empty_dv(s - 1, 3)
+            multiply_de(u + 1)
             multiply_dv(s, 1)
             back(u)
-            empty_dv(s, 0)
             multiply_dv(s, 2)
-            empty_dv(s, 1)
             multiply_dv(s, 3)
-            empty_dv(s, 2)
-            empty_dv(s, 3)
+            sum_next(len(pending))
+            for m in range(J):
+                empty_dv(s, m)
             add_row_gpsimd(s, "dz_il%d" % ((s - 1) % 2))
             back(u + 1)
             merge(2)

@@ -13,6 +13,7 @@ ADD = mybir.AluOpType.add
 MULT = mybir.AluOpType.mult
 SUBTRACT = mybir.AluOpType.subtract
 EXP = mybir.ActivationFunctionType.Exp
+IDENTITY = mybir.ActivationFunctionType.Identity
 
 P = 128
 J = 4
@@ -40,7 +41,6 @@ def tile_single_head_split_window_attention_1d_v_kernel(
         psum = ctx.enter_context(tc.psum_pool(name="psum", bufs=1))
 
         ident = keep.tile([P, P], F32, name="ident")
-        warm = keep.tile([P, 1], F32, name="warm")
         rmax = keep.tile([P, len(steps), 2 * J], F32, name="rmax")
         neg_max = keep.tile([P, len(steps), J], F32, name="neg_max")
         mask = [keep.tile([P, J, WIN], BF16, name="mask%d" % n) for n in range(SPLITS)]
@@ -309,9 +309,7 @@ def tile_single_head_split_window_attention_1d_v_kernel(
         make_identity(nc, ident[:])
         with tc.manual_schedule():
             load_row_max(0, 1, nc.scalar)
-            negate_row_max(0, 1, nc.gpsimd)
-            nc.vector.memset(warm[:], 0.0)
-            nc.scalar.activation(out=warm[:], in_=warm[:], func=EXP)
+            nc.scalar.activation(out=neg_max[:, 0, :], in_=rmax[:, 0, 0:J], func=IDENTITY, scale=-1.0)
             for j in range(J):
                 load_scores(0, j, j + 1)
             load_v(0)

@@ -72,9 +72,10 @@ def tile_single_head_split_window_attention_1d_v_kernel(
                 tiles[i]["e"] = keep.tile([P, J, WIN], F32, name="e%d" % i)
             src = scores[r, n].rearrange("(p j) k -> p j k", j=J)
             nc.sync.dma_start(out=tiles[i]["e"][:, a:b, :], in_=src[:, a:b, :])
-            if r == 0:
-                msrc = attn_mask[n].rearrange("(p j) k -> p j k", j=J)
-                nc.sync.dma_start(out=mask[n][:, a:b, :], in_=msrc[:, a:b, :])
+
+        def load_mask(n, a, b):
+            src = attn_mask[n].rearrange("(p j) k -> p j k", j=J)
+            nc.sync.dma_start(out=mask[n][:, a:b, :], in_=src[:, a:b, :])
 
         def load_grad(i, a, b):
             n, r = steps[i]
@@ -84,13 +85,16 @@ def tile_single_head_split_window_attention_1d_v_kernel(
                 src = image(grad_out, r)[x0 : x0 + rows, :].rearrange("(p j) c -> p j c", j=J)
                 nc.sync.dma_start(out=tiles[i]["g"][win0 // J : (win0 + rows) // J, a:b, :], in_=src[:, a:b, :])
 
-        def load_v(i):
+        def load_v(i, a=0, b=2):
             n, r = steps[i]
-            t = keep.tile([P, J, C], BF16, name="v%d" % i)
-            tiles[i]["v"] = t
+            if a == 0:
+                tiles[i]["v"] = keep.tile([P, J, C], BF16, name="v%d" % i)
+            t = tiles[i]["v"]
             for win0, x0, rows in spans(n, r):
-                src = image(v, r)[x0 : x0 + rows, :].rearrange("(t p) c -> p t c", p=P)
-                nc.sync.dma_start(out=t[:, win0 // P : (win0 + rows) // P, :], in_=src)
+                lo, hi = max(win0, a * 2 * P), min(win0 + rows, b * 2 * P)
+                if lo < hi:
+                    src = image(v, r)[x0 + lo - win0 : x0 + hi - win0, :].rearrange("(b p t) c -> p b (t c)", p=P, t=2)
+                    nc.sync.dma_start(out=t[:].rearrange("p (b t) c -> p b (t c)", t=2)[:, lo // (2 * P) : hi // (2 * P), :], in_=src)
 
         def add_mask_vector(i, a, b):
             e, m = tiles[i]["e"], mask[steps[i][0]]
@@ -180,8 +184,9 @@ def tile_single_head_split_window_attention_1d_v_kernel(
                     nc.tensor.transpose(ps[:, a, u, :], words[:, 2 * b + a, picked], ident[:])
 
         def unload(i, name, b, dst):
-            words = dst.rearrange("p x j -> p (x j)").bitcast(F32).rearrange("p (a x u) -> p a x u", a=2, u=2)
-            nc.scalar.copy(out=words, in_=tiles[i][name, b][:].rearrange("p a u x -> p a x u"))
+            order = "x a u" if name == "v" else "a x u"
+            words = dst.rearrange("p x j -> p (x j)").bitcast(F32).rearrange("p (%s) -> p %s" % (order, order), a=2, u=2)
+            nc.scalar.copy(out=words, in_=tiles[i][name, b][:].rearrange("p a u x -> p " + order))
 
         def turn_dz(u):
             turn(u // 2, "dz", u % 2)
@@ -222,7 +227,7 @@ def tile_single_head_split_window_attention_1d_v_kernel(
         def empty_dv(i, m):
             n, r = steps[i]
             if m == 0:
-                tiles[i]["dv_sb"] = work.tile([P, J, C], F32, name="dv_sb")
+                tiles[i]["dv_sb"] = work.tile([P, J, C], F32, name="dv_sb", bufs=3)
             sb = tiles[i]["dv_sb"]
             nc.scalar.copy(
                 out=sb[:, m, :].rearrange("p (x u e) -> p x u e", u=2, e=2),
@@ -311,6 +316,8 @@ def tile_single_head_split_window_attention_1d_v_kernel(
             load_row_max(0, 1, nc.scalar)
             nc.scalar.activation(out=neg_max[:, 0, :], in_=rmax[:, 0, 0:J], func=IDENTITY, scale=-1.0)
             for j in range(J):
+                if j % 2 == 0:
+                    load_mask(0, j, j + 2)
                 load_scores(0, j, j + 1)
             load_v(0)
             load_grad(0, 0, 2)
@@ -323,6 +330,9 @@ def tile_single_head_split_window_attention_1d_v_kernel(
             load_scores(2, 0, J)
             load_row_max(2, ROWS, nc.sync)
             load_row_max(ROWS, 2 * ROWS, nc.sync)
+            load_v(2)
+            load_grad(2, 0, J)
+            load_scores(3, 0, J)
 
             for j in range(J):
                 add_mask_vector(0, j, j + 1)
@@ -354,9 +364,11 @@ def tile_single_head_split_window_attention_1d_v_kernel(
 
             for s in range(last):
                 u = 2 * s
-                step(s + 2, load_v)
-                step(s + 2, load_grad, 0, J)
-                step(s + 3, load_scores, 0, J)
+                step(s + 3, load_v)
+                step(s + 3, load_grad, 0, J)
+                if s == 0:
+                    load_mask(1, 0, J)
+                step(s + 4, load_scores, 0, J)
                 unit(u + 3, add_mask_gpsimd, "dz_il%d" % ((s - 1) % 2) if s else "e_il0")
                 sum_next()
                 interleave_dz(s, 0)

@@ -14,6 +14,7 @@ MULT = mybir.AluOpType.mult
 SUBTRACT = mybir.AluOpType.subtract
 EXP = mybir.ActivationFunctionType.Exp
 IDENTITY = mybir.ActivationFunctionType.Identity
+COPY = mybir.ActivationFunctionType.Copy
 
 P = 128
 J = 4
@@ -21,6 +22,11 @@ WIN = 512
 C = 512
 ROWS = 4
 SPLITS = 2
+DVB = 3
+VS5 = 128
+VS = 0
+K1 = 0
+VL = 256
 
 FLOPS = 2 * ROWS * SPLITS * 2 * WIN * WIN * C
 BYTES = 4 * ROWS * SPLITS * WIN * WIN + 2 * 2 * (ROWS * SPLITS * WIN * C) + 2 * SPLITS * WIN * WIN + 4 * ROWS * SPLITS * WIN * C + 4 * SPLITS * WIN * WIN
@@ -41,12 +47,13 @@ def tile_single_head_split_window_attention_1d_v_kernel(
         psum = ctx.enter_context(tc.psum_pool(name="psum", bufs=1))
 
         ident = keep.tile([P, P], F32, name="ident")
+        minus = keep.tile([P, P], F32, name="minus")
         rmax = keep.tile([P, len(steps), 2 * J], F32, name="rmax")
         neg_max = keep.tile([P, len(steps), J], F32, name="neg_max")
         mask = [keep.tile([P, J, WIN], BF16, name="mask%d" % n) for n in range(SPLITS)]
         tiles = [dict() for s in steps]
-        units = [dict() for u in range(2 * len(steps))]
         sums = {}
+        pending = []
 
         def image(x, r):
             return x[r // h]
@@ -85,175 +92,157 @@ def tile_single_head_split_window_attention_1d_v_kernel(
                 src = image(grad_out, r)[x0 : x0 + rows, :].rearrange("(p j) c -> p j c", j=J)
                 nc.sync.dma_start(out=tiles[i]["g"][win0 // J : (win0 + rows) // J, a:b, :], in_=src[:, a:b, :])
 
-        def load_v(i, a=0, b=2):
+        def load_v(i):
             n, r = steps[i]
-            if a == 0:
-                tiles[i]["v"] = keep.tile([P, J, C], BF16, name="v%d" % i)
-            t = tiles[i]["v"]
+            t = keep.tile([P, J, C], BF16, name="v%d" % i)
+            tiles[i]["v"] = t
             for win0, x0, rows in spans(n, r):
-                lo, hi = max(win0, a * 2 * P), min(win0 + rows, b * 2 * P)
-                if lo < hi:
-                    src = image(v, r)[x0 + lo - win0 : x0 + hi - win0, :].rearrange("(b p t) c -> p b (t c)", p=P, t=2)
-                    nc.sync.dma_start(out=t[:].rearrange("p (b t) c -> p b (t c)", t=2)[:, lo // (2 * P) : hi // (2 * P), :], in_=src)
+                src = image(v, r)[x0 : x0 + rows, :].rearrange("(t p) c -> p t c", p=P)
+                nc.sync.dma_start(out=t[:, win0 // P : (win0 + rows) // P, :], in_=src)
 
-        def add_mask_vector(i, a, b):
-            e, m = tiles[i]["e"], mask[steps[i][0]]
-            nc.vector.tensor_tensor(out=e[:, a:b, :], in0=e[:, a:b, :], in1=m[:, a:b, :], op=ADD)
-            for j in range(a, b):
-                tiles[i]["t", j] = e[:, j, :]
+        def add_mask_vector(i, j):
+            e = tiles[i]["e"][:, j, :]
+            nc.vector.tensor_tensor(out=e, in0=e, in1=mask[steps[i][0]][:, j, :], op=ADD)
+            tiles[i]["t", j] = e
 
-        def add_mask_gpsimd(u, tag):
-            i, half = divmod(u, 2)
+        def add_mask_gpsimd(i, half):
             e, m = tiles[i]["e"], mask[steps[i][0]]
-            t = work.tile([P, 2, WIN], F32, name="t", tag=tag, bufs=1, align_bytes=64)
             js = slice(2 * half, 2 * half + 2)
-            nc.gpsimd.tensor_tensor(out=t[:], in0=e[:, js, :], in1=m[:, js, :], op=ADD)
+            if half == 0:
+                t = e[:, js, :]
+            else:
+                t = work.tile([P, 2, WIN], F32, name="t", tag="v_t%d" % (i % 2) if i > 1 else "dz_t0", bufs=1, align_bytes=64)[:]
+            nc.gpsimd.tensor_tensor(out=t, in0=e[:, js, :], in1=m[:, js, :], op=ADD)
             for a in range(2):
                 tiles[i]["t", 2 * half + a] = t[:, a, :]
 
-        def exponential(u, a):
-            i, half = divmod(u, 2)
-            j = 2 * half + a
-            if a == 0:
-                units[u]["z"] = small.tile([P, 2], F32, name="z")
+        def exponential(i, j):
+            if j % 2 == 0:
+                tiles[i]["z", j // 2] = small.tile([P, 2], F32, name="z")
             nc.scalar.activation(
                 out=tiles[i]["e"][:, j, :], in_=tiles[i]["t", j], func=EXP, bias=neg_max[:, i, j : j + 1],
-                accum_out=units[u]["z"][:, a : a + 1],
+                accum_out=tiles[i]["z", j // 2][:, j % 2 : j % 2 + 1],
             )
 
-        def invert(u):
-            units[u]["rz"] = small.tile([P, 2], F32, name="rz")
-            nc.vector.reciprocal(out=units[u]["rz"][:], in_=units[u]["z"][:])
+        def invert(i, half):
+            rz = small.tile([P, 2], F32, name="rz", bufs=6)
+            nc.vector.reciprocal(out=rz[:], in_=tiles[i]["z", half][:])
+            for a in range(2):
+                tiles[i]["rz", 2 * half + a] = rz[:, a : a + 1]
 
-        def scale(u):
-            i, half = divmod(u, 2)
+        def scale(i, half):
             if half == 0:
                 tiles[i]["dz"] = work.tile([P, J, C], BF16, name="dz", align_bytes=64)
-            for a in range(2):
-                j = 2 * half + a
+            for j in range(2 * half, 2 * half + 2):
                 nc.vector.tensor_scalar(
                     out=tiles[i]["dz"][:, j, :].rearrange("p (u x e) -> p u x e", u=2, e=2),
-                    in0=tiles[i]["g"][:, j, :].rearrange("p (x u e) -> p u x e", u=2, e=2), scalar1=units[u]["rz"][:, a : a + 1], scalar2=None, op0=MULT
+                    in0=tiles[i]["g"][:, j, :].rearrange("p (x u e) -> p u x e", u=2, e=2), scalar1=tiles[i]["rz", j], scalar2=None, op0=MULT
                 )
 
-        def four_by_four(dst, src, cols, run=4):
+        def staging(i, name):
+            t = tiles[i]
+            if name not in t:
+                t[name] = work.tile([P, J * WIN], BF16, name=name, tag="%s%d" % (name, i % 2), bufs=1, align_bytes=64)
+            return t[name]
+
+        def quantise(i, name, a=0, b=2):
+            t = tiles[i]
+            if a == 0:
+                t[name, "q"] = work.tile([P, WIN], U32, name=name + "_q", align_bytes=64)
+                t[name, "s"] = work.tile([P, WIN], U8, name=name + "_s", align_bytes=64)
+            fmt = E5M2X4 if name in ("dz_t", "dz_il") else E4M3X4
+            a, b = a * 2 * P, b * 2 * P
+            nc.vector.quantize_mx(out=t[name, "q"][:, a:b].bitcast(fmt), scales=t[name, "s"][:, a:b], in_=t[name][:, J * a : J * b])
+
+        def interleaved(dst, src, cols, run):
             return dict(
-                out=dst[:, cols, :].rearrange("p (c i) j -> p c j i", i=run),
+                out=dst.rearrange("p (c j) -> p c j", j=J)[:, cols, :].rearrange("p (c i) j -> p c j i", i=run),
                 in_=src[:, :, cols].rearrange("p j (c i) -> p c j i", i=run),
             )
 
-        def interleave_e(i):
-            tiles[i]["e_il"] = work.tile([P, WIN, J], BF16, name="e_il", tag="e_il%d" % (i % 2), bufs=1, align_bytes=64)
-            nc.vector.tensor_copy(**four_by_four(tiles[i]["e_il"], tiles[i]["e"], slice(0, WIN), 2))
+        def interleave_e(engine, i, a, b):
+            if a < b:
+                engine(**interleaved(staging(i, "e_il")[:], tiles[i]["e"], slice(a, b), 2 if engine is on_vector else 4))
 
-        def interleave_dz(i, part):
-            if part == 0:
-                tiles[i]["dz_il"] = work.tile([P, C, J], BF16, name="dz_il", tag="dz_il%d" % (i % 2), bufs=1, align_bytes=64)
-            if part < scalar_parts(i):
-                nc.scalar.copy(**four_by_four(tiles[i]["dz_il"], tiles[i]["dz"], slice(part * P, (part + 1) * P)))
+        def interleave_dz(engine, i, a, b):
+            if a < b:
+                engine(**interleaved(staging(i, "dz_il")[:], tiles[i]["dz"], slice(a, b), 4))
 
-        def scalar_parts(i):
-            return {0: 3, ROWS + 1: 3, last: 2}.get(i, 4)
+        def vector_share(i):
+            return {ROWS + 1: VS5}.get(i, VS)
 
-        def interleave_dz_rest(i):
-            if scalar_parts(i) < 4:
-                nc.vector.tensor_copy(**four_by_four(tiles[i]["dz_il"], tiles[i]["dz"], slice(scalar_parts(i) * P, C)))
+        def scalar_keys(i):
+            return {1: K1}.get(i, 0)
 
-        def quantise(held, name, fmt):
-            src = held[name][:].rearrange("p a b -> p (a b)")
-            width = src.shape[1] // J
-            codes = work.tile([P, width], U32, name=name + "_q", align_bytes=64)
-            scl = work.tile([P, width], U8, name=name + "_s", align_bytes=64)
-            held[name, "q"] = codes[:].bitcast(fmt)
-            held[name, "s"] = scl
-            nc.vector.quantize_mx(out=codes[:].bitcast(fmt), scales=scl[:], in_=src)
+        on_vector, on_scalar = nc.vector.tensor_copy, nc.scalar.copy
 
-        def quantise_step(i, name, fmt):
-            quantise(tiles[i], name, fmt)
-
-        def quantise_dz_t(u):
-            quantise(units[u], "dz_t", E5M2X4)
-
-        def turn(i, name, b):
+        def turn(i, name, b, bank):
             words = tiles[i][name][:].rearrange("p a c -> p (a c)").bitcast(F32).rearrange("p (a c) -> p a c", a=J)
-            ps = psum.tile([P, 2, 2, P], F32, name="turn", tag="bank", bufs=2)
+            ps = psum.tile([P, 2, 2, P], F32, name="turn", tag=bank)
             tiles[i][name, b] = ps
             for a in range(2):
                 for u in range(2):
                     picked = slice(u, C // 2, 2) if name == "v" else slice(u * P, (u + 1) * P)
                     nc.tensor.transpose(ps[:, a, u, :], words[:, 2 * b + a, picked], ident[:])
 
-        def unload(i, name, b, dst):
-            order = "x a u" if name == "v" else "a x u"
-            words = dst.rearrange("p x j -> p (x j)").bitcast(F32).rearrange("p (%s) -> p %s" % (order, order), a=2, u=2)
-            nc.scalar.copy(out=words, in_=tiles[i][name, b][:].rearrange("p a u x -> p " + order))
+        def unload(i, name, b):
+            dst = staging(i, name + "_t")
+            words = dst[:, 2 * J * P * b : 2 * J * P * (b + 1)].bitcast(F32).rearrange("p (a x u) -> p a x u", a=2, u=2)
+            nc.scalar.copy(out=words, in_=tiles[i][name, b][:].rearrange("p a u x -> p a x u"))
 
-        def turn_dz(u):
-            turn(u // 2, "dz", u % 2)
-
-        def unload_dz(u):
-            units[u]["dz_t"] = work.tile([P, 2 * P, J], BF16, name="dz_t", align_bytes=64)
-            unload(u // 2, "dz", u % 2, units[u]["dz_t"][:])
-
-        def unload_v(i, b):
-            if b == 0:
-                tiles[i]["v_t"] = work.tile([P, WIN, J], BF16, name="v_t", tag="v_t%d" % (i % 2), bufs=1, align_bytes=64)
-            unload(i, "v", b, tiles[i]["v_t"][:, 2 * P * b : 2 * P * (b + 1), :])
-
-        def multiply_de(u):
-            t = tiles[u // 2]
-            for a in range(2):
-                if u < len(units) - 1:
-                    ps = psum.tile([P, WIN], F32, name="de", bufs=2)
-                else:
-                    ps = psum.tile([P, WIN], F32, name="de_last", tag="sum", bufs=J)
-                units[u]["de", a] = ps
-                cols = slice(P * a, P * (a + 1))
-                nc.tensor.matmul_mx(
-                    out=ps[:], lhsT=units[u]["dz_t", "q"][:, cols], lhsT_scale=units[u]["dz_t", "s"][:, cols], rhs=t["v_t", "q"],
-                    rhs_scale=t["v_t", "s"][:], start=True, stop=True,
-                )
-
-        def multiply_dv(i, m):
+        def multiply_de(i, j, bank):
             t = tiles[i]
-            ps = psum.tile([P, C], F32, name="dv", tag="de" if i == last and m >= 2 else "bank", bufs=2)
-            t["dv", m] = ps
+            t["de", j] = psum.tile([P, WIN], F32, name="de", tag=bank)
+            cols = slice(P * j, P * (j + 1))
+            nc.tensor.matmul_mx(
+                out=t["de", j][:], lhsT=t["dz_t", "q"][:, cols].bitcast(E5M2X4), lhsT_scale=t["dz_t", "s"][:, cols],
+                rhs=t["v_t", "q"][:].bitcast(E4M3X4), rhs_scale=t["v_t", "s"][:], start=True, stop=True,
+            )
+
+        def multiply_dv(i, m, bank):
+            t = tiles[i]
+            t["dv", m] = psum.tile([P, C], F32, name="dv", tag=bank)
             cols = slice(P * m, P * (m + 1))
             nc.tensor.matmul_mx(
-                out=ps[:], lhsT=t["e_il", "q"][:, cols], lhsT_scale=t["e_il", "s"][:, cols], rhs=t["dz_il", "q"], rhs_scale=t["dz_il", "s"][:],
-                start=True, stop=True,
+                out=t["dv", m][:], lhsT=t["e_il", "q"][:, cols].bitcast(E4M3X4), lhsT_scale=t["e_il", "s"][:, cols],
+                rhs=t["dz_il", "q"][:].bitcast(E5M2X4), rhs_scale=t["dz_il", "s"][:], start=True, stop=True,
             )
 
         def empty_dv(i, m):
             n, r = steps[i]
             if m == 0:
-                tiles[i]["dv_sb"] = work.tile([P, J, C], F32, name="dv_sb", bufs=3)
+                tiles[i]["dv_sb"] = work.tile([P, J, C], F32, name="dv_sb", bufs=DVB)
             sb = tiles[i]["dv_sb"]
             nc.scalar.copy(
                 out=sb[:, m, :].rearrange("p (x u e) -> p x u e", u=2, e=2),
                 in_=tiles[i]["dv", m][:].rearrange("p (u x e) -> p x u e", u=2, e=2),
             )
-            count = 1 if i == last else 2
+            count = 1 if i >= last - 1 else 2
             if (m + 1) % count == 0:
                 m0 = m + 1 - count
                 x0 = [x0 + P * m0 - win0 for win0, x0, rows in spans(n, r) if win0 <= P * m0 < win0 + rows][0]
                 dst = image(out_0, r)[x0 : x0 + count * P, :].rearrange("(t p) c -> p t c", p=P)
                 nc.sync.dma_start(out=dst, in_=sb[:, m0 : m + 1, :])
 
-        def weigh(u, a):
-            if a == 0:
-                units[u]["dot"] = small.tile([P, 2], F32, name="dot")
-            t = units[u]
-            waste = work.tile([P, WIN], F32, name="waste")
+        def folded(i, j):
+            return steps[i][1] == ROWS - 1 and j < 2
+
+        def weigh(i, j):
+            t = tiles[i]
+            t["dot", j] = small.tile([P, 1], F32, name="dot", bufs=6)
+            t["prod", j] = work.tile([P, WIN], F32, name="prod", tag="prod" if folded(i, j) else "waste")
             nc.vector.scalar_tensor_tensor(
-                out=waste[:], in0=t["de", a][:], scalar=t["rz"][:, a : a + 1], in1=tiles[u // 2]["e"][:, 2 * (u % 2) + a, :],
-                op0=MULT, op1=MULT, accum_out=t["dot"][:, a : a + 1],
+                out=t["prod", j][:], in0=t["de", j][:], scalar=-1.0 if folded(i, j) else t["rz", j], in1=t["e"][:, j, :],
+                op0=MULT, op1=MULT, accum_out=t["dot", j][:],
             )
 
-        def subtract(u, a):
-            t = units[u]
-            e = tiles[u // 2]["e"][:, 2 * (u % 2) + a, :]
-            nc.vector.scalar_tensor_tensor(out=e, in0=t["de", a][:], scalar=t["dot"][:, a : a + 1], in1=e, op0=SUBTRACT, op1=MULT)
+        def subtract(i, j):
+            t = tiles[i]
+            e = t["e"][:, j, :]
+            nc.vector.scalar_tensor_tensor(out=e, in0=t["de", j][:], scalar=t["dot", j][:], in1=e, op0=SUBTRACT, op1=MULT)
+            if i < ROWS or j < 2:
+                pending.extend((i, j, b) for b in range(2))
+                pending.sort(key=lambda x: (x[0] // ROWS, x[1] >= 2, x[0], x[1], x[2]))
 
         def store_sum(n, j, src):
             nc.sync.dma_start(out=out_1[n].rearrange("(p j) k -> p j k", j=J)[:, j, :], in_=src)
@@ -262,57 +251,221 @@ def tile_single_head_split_window_attention_1d_v_kernel(
             for i, j, half in pending[:count]:
                 n, r = steps[i]
                 if r == 0 and half == 0:
-                    sums[n, j] = psum.tile([P, WIN], F32, name="sum", bufs=J)
+                    sums[n, j] = psum.tile([P, WIN], F32, name="sum", tag="sum%d" % j)
                 cols = slice(half * WIN // 2, (half + 1) * WIN // 2)
                 nc.tensor.matmul(
                     out=sums[n, j][:, cols], lhsT=ident[:], rhs=tiles[i]["e"][:, j, cols],
-                    start=(r == 0 and half == 0), stop=(r == ROWS - 1 - n and half == 1),
+                    start=(r == 0 and half == 0), stop=(r == ROWS - 1 and half == 1),
                 )
             pending[:count] = []
 
+        def sum_product(i, j):
+            t = tiles[i]
+            assert all(x[1] != j for x in pending)
+            nc.tensor.matmul(out=sums[steps[i][0], j][:], lhsT=minus[:], rhs=t["prod", j][:], start=False, stop=True)
+
+        def factor(i, j):
+            t = tiles[i]
+            t["factor", j] = small.tile([P, 1], F32, name="factor")
+            nc.scalar.activation(out=t["factor", j][:], in_=t["dot", j][:], func=COPY, scale=t["rz", j])
+
+        def finish(i, j):
+            t = tiles[i]
+            e = t["e"][:, j, :]
+            nc.vector.scalar_tensor_tensor(out=e, in0=e, scalar=t["factor", j][:], in1=sums[steps[i][0], j][:], op0=MULT, op1=ADD)
+            store_sum(steps[i][0], j, e)
+
         def empty_sum(j):
+            assert all(x[1] != j for x in pending if x[0] < ROWS)
             ds = tiles[ROWS - 1]["e"]
             nc.scalar.copy(out=ds[:, j, :], in_=sums[0, j][:])
             store_sum(0, j, ds[:, j, :])
 
-        def merge(j):
-            ds = tiles[last]["e"]
-            nc.vector.tensor_tensor(out=ds[:, j, :], in0=sums[1, j][:], in1=ds[:, j, :], op=ADD)
-            store_sum(1, j, ds[:, j, :])
-
-        def add_row_gpsimd(i, tag):
-            total = work.tile([P, 2, WIN], F32, name="total", tag=tag, bufs=1, align_bytes=64)
-            before = sums.get("gpsimd", tiles[ROWS]["e"])
-            if i < last:
-                nc.gpsimd.tensor_tensor(out=total[:], in0=before[:, 0:2, :], in1=tiles[i]["e"][:, 0:2, :], op=ADD)
+        def add_row_gpsimd(i):
+            if i == ROWS + 1:
+                total = work.tile([P, 2, WIN], F32, name="total", bufs=1)[:]
+                before = tiles[ROWS]["e"][:, 2:J, :]
             else:
-                for j in range(2):
-                    nc.gpsimd.tensor_tensor(out=total[:, j, :], in0=before[:, j, :], in1=tiles[i]["e"][:, j, :], op=ADD)
-                    store_sum(1, j, total[:, j, :])
+                total = work.tile([P, 2, WIN], F32, name="total", tag="dz_il%d" % (last % 2), bufs=1, align_bytes=64)[:]
+                before = sums["gpsimd"]
+            nc.gpsimd.tensor_tensor(out=total, in0=before, in1=tiles[i]["e"][:, 2:J, :], op=ADD)
             sums["gpsimd"] = total
 
-        pending = []
-
-        def back(u):
-            i, half = divmod(u, 2)
-            weigh(u, 0)
-            weigh(u, 1)
-            unit(u + 2, invert)
-            for a in range(2):
-                subtract(u, a)
-                if i < ROWS or (half == 1 and i < last):
-                    pending.extend((i, 2 * half + a, b) for b in range(2))
+        def add_last_row(engine, j, a, b):
+            ds = tiles[last]["e"][:, j, a:b]
+            engine.tensor_tensor(out=ds, in0=sums["gpsimd"][:, j - 2, a:b], in1=ds, op=ADD)
+            nc.sync.dma_start(out=out_1[1].rearrange("(p j) k -> p j k", j=J)[:, j, a:b], in_=ds)
 
         def step(i, op, *args):
             if 0 <= i <= last:
                 op(i, *args)
 
-        def unit(u, op, *args):
-            if u < len(units):
-                op(u, *args)
+        def forward(s):
+            if s == 1:
+                scale(1, 0)
+                turn(1, "dz", 0, "d")
+            else:
+                quantise(s, "dz_t", 0, 1)
+            scale(s, 1)
+            turn(s, "dz", 1, "a")
+            if s == 1:
+                negate_row_max(2, ROWS, nc.vector)
+                exponential(2, 0)
+                unload(1, "dz", 0)
+                unload(1, "dz", 1)
+                exponential(2, 1)
+                quantise(1, "v_t")
+            else:
+                exponential(s + 1, 0)
+                exponential(s + 1, 1)
+                unload(s, "dz", 1)
+            if s == 2:
+                negate_row_max(ROWS, 2 * ROWS, nc.vector)
+            unload(s + 1, "v", 1)
+            interleave_dz(on_vector, s - 1, C - vector_share(s - 1), C)
+            interleave_e(on_vector, s, scalar_keys(s), WIN)
+            quantise(s - 1, "dz_il")
+            if s == 1:
+                quantise(s, "dz_t", 0, 1)
+            sum_next(2)
+            multiply_dv(s - 1, 0, "d")
+            multiply_dv(s - 1, 1, "c")
+            multiply_de(s, 0, "a")
+            multiply_de(s, 1, "b")
+            sum_next()
+            invert(s + 1, 0)
+            quantise(s, "dz_t", 1, 2)
+            scale(s + 1, 0)
+            interleave_dz(on_scalar, s, 0, P)
+            empty_dv(s - 1, 0)
+            empty_dv(s - 1, 1)
+            turn(s + 1, "dz", 0, "d")
+            multiply_de(s, 2, "c")
+            quantise(s + 1, "v_t")
+            quantise(s, "e_il")
+
+        def backward(s):
+            add_mask_gpsimd(s + 1, 1)
+            step(s + 2, add_mask_gpsimd, 0)
+            if s == last - 1:
+                add_row_gpsimd(s - 1)
+            fold = folded(s, 0)
+            if s == 0:
+                interleave_dz(on_scalar, s, 0, 2 * P)
+                unload(1, "v", 0)
+                turn(1, "v", 1, "sum3")
+                unload(1, "v", 1)
+            else:
+                interleave_dz(on_scalar, s, P, 2 * P)
+                unload(s + 1, "dz", 0)
+            weigh(s, 0)
+            if fold:
+                sum_next(len([x for x in pending if x[1] < 2]))
+                multiply_de(s, 3, "a")
+                sum_product(s, 0)
+            else:
+                sum_next()
+            step(s - 1, multiply_dv, 2, "d")
+            weigh(s, 1)
+            if s == 0:
+                invert(1, 0)
+            if s:
+                interleave_dz(on_scalar, s, 2 * P, C - vector_share(s))
+            if fold:
+                factor(s, 0)
+                factor(s, 1)
+            step(s - 1, empty_dv, 2)
+            if fold:
+                sum_product(s, 1)
+                weigh(s, 2)
+                weigh(s, 3)
+            else:
+                subtract(s, 0)
+                multiply_de(s, 3, "a")
+                weigh(s, 2)
+                subtract(s, 1)
+                sum_next(2 if s == last - 1 else 1)
+            step(s - 1, multiply_dv, 3, "d")
+            step(s + 2, turn, "v", 0, "b")
+            exponential(s + 1, 2)
+            exponential(s + 1, 3)
+            if s == 0:
+                interleave_e(on_scalar, 1, 0, scalar_keys(1))
+                interleave_dz(on_scalar, s, 2 * P, C)
+            if fold:
+                subtract(s, 2)
+                subtract(s, 3)
+            else:
+                weigh(s, 3)
+                subtract(s, 2)
+            sum_next(2 if s == last - 1 else 1)
+            step(s + 2, turn, "v", 1, "c")
+            step(s - 1, empty_dv, 3)
+            step(s + 2, unload, "v", 0)
+            if s > ROWS:
+                empty_sum(s - ROWS + 1)
+            if fold:
+                finish(s, 0)
+                finish(s, 1)
+            else:
+                subtract(s, 3)
+            invert(s + 1, 1)
+
+        def finale(s):
+            quantise(s, "dz_t", 0, 1)
+            scale(s, 1)
+            turn(s, "dz", 1, "a")
+            quantise(s - 1, "dz_il")
+            sum_next()
+            multiply_dv(s - 1, 0, "c")
+            multiply_dv(s - 1, 1, "d")
+            multiply_dv(s - 1, 2, "b")
+            multiply_dv(s - 1, 3, "sum2")
+            sum_next(len(pending))
+            interleave_dz(on_scalar, s, 0, P)
+            unload(s, "dz", 1)
+            empty_dv(s - 1, 0)
+            interleave_e(on_vector, s, 0, WIN)
+            interleave_dz(on_scalar, s, P, C - VL)
+            interleave_dz(on_vector, s, C - VL, C)
+            for m in range(1, J):
+                empty_dv(s - 1, m)
+            multiply_de(s, 0, "sum3")
+            multiply_de(s, 1, "a")
+            quantise(s, "dz_t", 1, 2)
+            multiply_de(s, 2, "c")
+            quantise(s, "e_il")
+            quantise(s, "dz_il")
+
+            add_row_gpsimd(s - 1)
+            multiply_dv(s, 0, "d")
+            multiply_dv(s, 1, "b")
+            weigh(s, 0)
+            multiply_de(s, 3, "sum3")
+            multiply_dv(s, 2, "sum2")
+            sum_product(s, 0)
+            empty_dv(s, 0)
+            multiply_dv(s, 3, "d")
+            weigh(s, 2)
+            weigh(s, 1)
+            sum_product(s, 1)
+            subtract(s, 2)
+            empty_dv(s, 1)
+            factor(s, 0)
+            empty_dv(s, 2)
+            factor(s, 1)
+            empty_dv(s, 3)
+            weigh(s, 3)
+            finish(s, 0)
+            add_last_row(nc.gpsimd, 2, 0, WIN)
+            subtract(s, 3)
+            finish(s, 1)
+            add_last_row(nc.vector, 3, 0, WIN // 2)
+            add_last_row(nc.vector, 3, WIN // 2, WIN)
 
         make_identity(nc, ident[:])
         with tc.manual_schedule():
+            nc.gpsimd.tensor_scalar(out=minus[:], in0=ident[:], scalar1=-1.0, scalar2=0.0, op0=MULT, op1=ADD)
             load_row_max(0, 1, nc.scalar)
             nc.scalar.activation(out=neg_max[:, 0, :], in_=rmax[:, 0, 0:J], func=IDENTITY, scale=-1.0)
             for j in range(J):
@@ -324,147 +477,54 @@ def tile_single_head_split_window_attention_1d_v_kernel(
             load_grad(0, 2, J)
             load_row_max(1, 2, nc.sync)
             load_scores(1, 0, 2)
-            load_v(1)
             load_scores(1, 2, J)
+            load_scores(2, 0, 2)
+            load_v(1)
             load_grad(1, 0, J)
-            load_scores(2, 0, J)
             load_row_max(2, ROWS, nc.sync)
-            load_row_max(ROWS, 2 * ROWS, nc.sync)
             load_v(2)
             load_grad(2, 0, J)
+            load_scores(2, 2, J)
+            load_row_max(ROWS, 2 * ROWS, nc.sync)
             load_scores(3, 0, J)
 
             for j in range(J):
-                add_mask_vector(0, j, j + 1)
-                exponential(j // 2, j % 2)
-            turn(0, "v", 0)
-            turn(0, "v", 1)
-            invert(0)
-            invert(1)
-            scale(0)
-            unload_v(0, 0)
-            turn_dz(0)
-            unload_v(0, 1)
-            interleave_e(0)
-            scale(1)
-            turn_dz(1)
-            unload_dz(0)
+                add_mask_vector(0, j)
+                exponential(0, j)
+            turn(0, "v", 0, "c")
+            turn(0, "v", 1, "d")
+            invert(0, 0)
+            invert(0, 1)
+            scale(0, 0)
+            unload(0, "v", 0)
+            turn(0, "dz", 0, "a")
+            unload(0, "v", 1)
+            interleave_e(on_vector, 0, 0, WIN)
+            scale(0, 1)
+            turn(0, "dz", 1, "b")
+            unload(0, "dz", 0)
+            unload(0, "dz", 1)
             negate_row_max(1, 2, nc.vector)
-            add_mask_vector(1, 0, 1)
-            quantise_step(0, "v_t", E4M3X4)
-            quantise_dz_t(0)
-            multiply_de(0)
-            exponential(2, 0)
-            unload_dz(1)
-            turn(1, "v", 0)
-            turn(1, "v", 1)
-            quantise_step(0, "e_il", E4M3X4)
-            add_mask_vector(1, 1, 2)
-            exponential(2, 1)
+            add_mask_vector(1, 0)
+            quantise(0, "v_t")
+            quantise(0, "dz_t", 0, 1)
+            multiply_de(0, 0, "a")
+            multiply_de(0, 1, "b")
+            exponential(1, 0)
+            add_mask_vector(1, 1)
+            quantise(0, "dz_t", 1, 2)
+            multiply_de(0, 2, "c")
+            exponential(1, 1)
+            quantise(0, "e_il")
+            turn(1, "v", 0, "d")
 
             for s in range(last):
-                u = 2 * s
                 step(s + 3, load_v)
                 step(s + 3, load_grad, 0, J)
                 if s == 0:
                     load_mask(1, 0, J)
                 step(s + 4, load_scores, 0, J)
-                unit(u + 3, add_mask_gpsimd, "dz_il%d" % ((s - 1) % 2) if s else "e_il0")
-                sum_next()
-                interleave_dz(s, 0)
-                unload_v(s + 1, 1 if s else 0)
-                step(s - 1, multiply_dv, 0)
-                sum_next()
-                interleave_dz(s, 1)
                 if s:
-                    unload_dz(u + 1)
-                else:
-                    unload_v(1, 1)
-                step(s - 1, multiply_dv, 1)
-                sum_next()
-                back(u)
-                step(s - 1, empty_dv, 0)
-                if s == ROWS + 1:
-                    empty_sum(0)
-
-                quantise_dz_t(u + 1)
-                multiply_de(u + 1)
-                step(s - 1, multiply_dv, 2)
-                scale(u + 2)
-                quantise_step(s + 1, "v_t", E4M3X4)
-                if s:
-                    quantise_step(s, "e_il", E4M3X4)
-                else:
-                    interleave_dz_rest(s)
-                unit(u + 4, add_mask_gpsimd, "v_t%d" % ((s + 1) % 2))
-                if s == last - 1:
-                    add_row_gpsimd(s - 1, "v_t%d" % ((s + 1) % 2))
-                exponential(u + 3, 0)
-                step(s - 1, empty_dv, 1)
-                turn_dz(u + 2)
-                sum_next(2)
-                exponential(u + 3, 1)
-                step(s - 1, empty_dv, 2)
-                step(s + 2, turn, "v", 0)
-                interleave_dz(s, 2)
-                unload_dz(u + 2)
-                step(s - 1, multiply_dv, 3)
-                if s == last - 1:
-                    sum_next(2)
-                interleave_dz(s, 3)
-                step(s + 2, unload_v, 0)
-                if s == ROWS + 2:
-                    empty_sum(2)
-                if s == ROWS + 1:
-                    empty_sum(1)
-                back(u + 1)
-
-                if s == 0:
-                    negate_row_max(2, len(steps), nc.vector)
-                quantise_dz_t(u + 2)
-                multiply_de(u + 2)
-                sum_next()
-                step(s + 2, turn, "v", 1)
-                if s:
-                    interleave_dz_rest(s)
-                scale(u + 3)
-                quantise_step(s, "dz_il", E5M2X4)
-                interleave_e(s + 1)
-                unit(u + 4, exponential, 0)
-                step(s - 1, empty_dv, 3)
-                turn_dz(u + 3)
-                unit(u + 4, exponential, 1)
-
-            s, u = last, 2 * last
-            multiply_dv(s - 1, 0)
-            sum_next()
-            empty_sum(3)
-            interleave_dz(s, 0)
-            unload_dz(u + 1)
-            interleave_dz(s, 1)
-            multiply_dv(s - 1, 1)
-            interleave_dz_rest(s)
-            quantise_dz_t(u + 1)
-            quantise_step(s, "e_il", E4M3X4)
-            quantise_step(s, "dz_il", E5M2X4)
-            add_row_gpsimd(s - 1, "e_il%d" % (s % 2))
-            empty_dv(s - 1, 0)
-            multiply_dv(s - 1, 2)
-            empty_dv(s - 1, 1)
-            multiply_dv(s - 1, 3)
-            sum_next()
-            empty_dv(s - 1, 2)
-            multiply_dv(s, 0)
-            empty_dv(s - 1, 3)
-            multiply_de(u + 1)
-            multiply_dv(s, 1)
-            back(u)
-            multiply_dv(s, 2)
-            multiply_dv(s, 3)
-            sum_next(len(pending))
-            for m in range(J):
-                empty_dv(s, m)
-            add_row_gpsimd(s, "dz_il%d" % ((s - 1) % 2))
-            back(u + 1)
-            merge(2)
-            merge(3)
+                    forward(s)
+                backward(s)
+            finale(last)

@@ -22,7 +22,7 @@ WIN = 512
 C = 512
 ROWS = 4
 SPLITS = 2
-DVB = 3
+DVB = 2
 VS5 = 128
 VS = 0
 K1 = 0
@@ -469,9 +469,8 @@ def tile_single_head_split_window_attention_1d_v_kernel(
             load_row_max(0, 1, nc.scalar)
             nc.scalar.activation(out=neg_max[:, 0, :], in_=rmax[:, 0, 0:J], func=IDENTITY, scale=-1.0)
             for j in range(J):
-                if j % 2 == 0:
-                    load_mask(0, j, j + 2)
                 load_scores(0, j, j + 1)
+                load_mask(0, j, j + 1)
             load_v(0)
             load_grad(0, 0, 2)
             load_grad(0, 2, J)
@@ -486,7 +485,6 @@ def tile_single_head_split_window_attention_1d_v_kernel(
             load_grad(2, 0, J)
             load_scores(2, 2, J)
             load_row_max(ROWS, 2 * ROWS, nc.sync)
-            load_scores(3, 0, J)
 
             for j in range(J):
                 add_mask_vector(0, j)
@@ -519,11 +517,12 @@ def tile_single_head_split_window_attention_1d_v_kernel(
             turn(1, "v", 0, "d")
 
             for s in range(last):
-                step(s + 3, load_v)
-                step(s + 3, load_grad, 0, J)
-                if s == 0:
+                if s:
+                    step(s + 2, load_v)
+                    step(s + 2, load_grad, 0, J)
+                step(s + 3, load_scores, 0, J)
+                if s == 1:
                     load_mask(1, 0, J)
-                step(s + 4, load_scores, 0, J)
                 if s:
                     forward(s)
                 backward(s)

@@ -162,7 +162,7 @@ def tile_single_head_split_window_attention_1d_v_kernel(
 
         def interleave_e(engine, i, a, b):
             if a < b:
-                engine(**interleaved(staging(i, "e_il")[:], tiles[i]["e"], slice(a, b), 2 if engine is on_vector else 4))
+                engine(**interleaved(staging(i, "e_il")[:], tiles[i]["e"], slice(a, b), 4))
 
         def interleave_dz(engine, i, a, b):
             if a < b:

@@ -25,6 +25,7 @@ SPLITS = 2
 DVB = 2
 VS5 = 128
 VS = 0
+K0 = 192
 K1 = 0
 VL = 256
 
@@ -491,29 +492,30 @@ def tile_single_head_split_window_attention_1d_v_kernel(
                 exponential(0, j)
             turn(0, "v", 0, "c")
             turn(0, "v", 1, "d")
+            interleave_e(on_scalar, 0, 0, K0)
             invert(0, 0)
             invert(0, 1)
+            interleave_e(on_vector, 0, K0, WIN)
             scale(0, 0)
-            unload(0, "v", 0)
             turn(0, "dz", 0, "a")
-            unload(0, "v", 1)
-            interleave_e(on_vector, 0, 0, WIN)
             scale(0, 1)
             turn(0, "dz", 1, "b")
+            unload(0, "v", 0)
+            unload(0, "v", 1)
+            nc.scalar.activation(out=neg_max[:, 1, :], in_=rmax[:, 1, 0:J], func=IDENTITY, scale=-1.0)
             unload(0, "dz", 0)
             unload(0, "dz", 1)
-            negate_row_max(1, 2, nc.vector)
-            add_mask_vector(1, 0)
+            quantise(0, "e_il")
             quantise(0, "v_t")
+            add_mask_vector(1, 0)
             quantise(0, "dz_t", 0, 1)
             multiply_de(0, 0, "a")
             multiply_de(0, 1, "b")
             exponential(1, 0)
-            add_mask_vector(1, 1)
             quantise(0, "dz_t", 1, 2)
+            add_mask_vector(1, 1)
             multiply_de(0, 2, "c")
             exponential(1, 1)
-            quantise(0, "e_il")
             turn(1, "v", 0, "d")
 
             for s in range(last):

@@ -26,6 +26,7 @@ DVB = 2
 VS5 = 128
 VS = 0
 K0 = 192
+EARLY = 128
 K1 = 0
 VL = 256
 
@@ -310,7 +311,7 @@ def tile_single_head_split_window_attention_1d_v_kernel(
             scale(s, 1)
             turn(s, "dz", 1, "a")
             if s == 1:
-                negate_row_max(2, ROWS, nc.vector)
+                nc.scalar.activation(out=neg_max[:, 2:ROWS, :], in_=rmax[:, 2:ROWS, 0:J], func=IDENTITY, scale=-1.0)
                 exponential(2, 0)
                 unload(1, "dz", 0)
                 unload(1, "dz", 1)
@@ -352,7 +353,7 @@ def tile_single_head_split_window_attention_1d_v_kernel(
                 add_row_gpsimd(s - 1)
             fold = folded(s, 0)
             if s == 0:
-                interleave_dz(on_scalar, s, 0, 2 * P)
+                interleave_dz(on_scalar, s, EARLY, 3 * P)
                 unload(1, "v", 0)
                 turn(1, "v", 1, "sum3")
                 unload(1, "v", 1)
@@ -392,7 +393,7 @@ def tile_single_head_split_window_attention_1d_v_kernel(
             exponential(s + 1, 3)
             if s == 0:
                 interleave_e(on_scalar, 1, 0, scalar_keys(1))
-                interleave_dz(on_scalar, s, 2 * P, C)
+                interleave_dz(on_scalar, s, 3 * P, C)
             if fold:
                 subtract(s, 2)
                 subtract(s, 3)
@@ -502,15 +503,16 @@ def tile_single_head_split_window_attention_1d_v_kernel(
             turn(0, "dz", 1, "b")
             unload(0, "v", 0)
             unload(0, "v", 1)
-            nc.scalar.activation(out=neg_max[:, 1, :], in_=rmax[:, 1, 0:J], func=IDENTITY, scale=-1.0)
             unload(0, "dz", 0)
+            nc.scalar.activation(out=neg_max[:, 1, :], in_=rmax[:, 1, 0:J], func=IDENTITY, scale=-1.0)
             unload(0, "dz", 1)
+            interleave_dz(on_scalar, 0, 0, EARLY)
             quantise(0, "e_il")
             quantise(0, "v_t")
-            add_mask_vector(1, 0)
             quantise(0, "dz_t", 0, 1)
             multiply_de(0, 0, "a")
             multiply_de(0, 1, "b")
+            add_mask_vector(1, 0)
             exponential(1, 0)
             quantise(0, "dz_t", 1, 2)
             add_mask_vector(1, 1)

from contextlib import ExitStack

import concourse.mybir as mybir
from concourse.masks import make_identity

F32 = mybir.dt.float32
BF16 = mybir.dt.bfloat16
U32 = mybir.dt.uint32
U8 = mybir.dt.uint8
E4M3X4 = mybir.dt.float8_e4m3fn_x4
E5M2X4 = mybir.dt.float8_e5m2_x4
ADD = mybir.AluOpType.add
MULT = mybir.AluOpType.mult
SUBTRACT = mybir.AluOpType.subtract
EXP = mybir.ActivationFunctionType.Exp
IDENTITY = mybir.ActivationFunctionType.Identity
COPY = mybir.ActivationFunctionType.Copy

P = 128
J = 4
WIN = 512
C = 512
ROWS = 4
SPLITS = 2
DVB = 2
VS5 = 128
VS = 0
K0 = 192
EARLY = 128
K1 = 0
VL = 256

FLOPS = 2 * ROWS * SPLITS * 2 * WIN * WIN * C
BYTES = 4 * ROWS * SPLITS * WIN * WIN + 2 * 2 * (ROWS * SPLITS * WIN * C) + 2 * SPLITS * WIN * WIN + 4 * ROWS * SPLITS * WIN * C + 4 * SPLITS * WIN * WIN


def tile_single_head_split_window_attention_1d_v_kernel(
    tc, q, k, v, attn_mask, h, w, num_splits, scores, row_max, grad_out, out_0, out_1
):
    nc = tc.nc
    assert (w, num_splits) == (SPLITS * WIN, SPLITS)
    steps = [(n, r) for n in range(SPLITS) for r in range(ROWS)]
    last = len(steps) - 1

    with ExitStack() as ctx:
        keep = ctx.enter_context(tc.tile_pool(name="keep", bufs=1))
        work = ctx.enter_context(tc.tile_pool(name="work", bufs=2))
        small = ctx.enter_context(tc.tile_pool(name="small", bufs=4))
        psum = ctx.enter_context(tc.psum_pool(name="psum", bufs=1))

        ident = keep.tile([P, P], F32, name="ident")
        minus = keep.tile([P, P], F32, name="minus")
        rmax = keep.tile([P, len(steps), 2 * J], F32, name="rmax")
        neg_max = keep.tile([P, len(steps), J], F32, name="neg_max")
        mask = [keep.tile([P, J, WIN], BF16, name="mask%d" % n) for n in range(SPLITS)]
        tiles = [dict() for s in steps]
        sums = {}
        pending = []

        def image(x, r):
            return x[r // h]

        def spans(n, r):
            first = (r % h) * w
            start = n * WIN + WIN // 2
            if start + WIN <= w:
                return [(0, first + start, WIN)]
            head = w - start
            return [(0, first + start, head), (head, first, WIN - head)]

        def load_row_max(a, b, queue):
            n, r0 = steps[a]
            queue.dma_start(out=rmax[:, a:b, 0:J], in_=row_max[r0 : r0 + b - a, n].rearrange("r (p j) -> p r j", j=J))

        def negate_row_max(a, b, engine):
            engine.tensor_scalar(out=neg_max[:, a:b, :], in0=rmax[:, a:b, 0:J], scalar1=-1.0, scalar2=0.0, op0=MULT, op1=ADD)

        def load_scores(i, a, b):
            n, r = steps[i]
            if a == 0:
                tiles[i]["e"] = keep.tile([P, J, WIN], F32, name="e%d" % i)
            src = scores[r, n].rearrange("(p j) k -> p j k", j=J)
            nc.sync.dma_start(out=tiles[i]["e"][:, a:b, :], in_=src[:, a:b, :])

        def load_mask(n, a, b):
            src = attn_mask[n].rearrange("(p j) k -> p j k", j=J)
            nc.sync.dma_start(out=mask[n][:, a:b, :], in_=src[:, a:b, :])

        def load_grad(i, a, b):
            n, r = steps[i]
            if a == 0:
                tiles[i]["g"] = keep.tile([P, J, C], BF16, name="g%d" % i)
            for win0, x0, rows in spans(n, r):
                src = image(grad_out, r)[x0 : x0 + rows, :].rearrange("(p j) c -> p j c", j=J)
                nc.sync.dma_start(out=tiles[i]["g"][win0 // J : (win0 + rows) // J, a:b, :], in_=src[:, a:b, :])

        def load_v(i):
            n, r = steps[i]
            t = keep.tile([P, J, C], BF16, name="v%d" % i)
            tiles[i]["v"] = t
            for win0, x0, rows in spans(n, r):
                src = image(v, r)[x0 : x0 + rows, :].rearrange("(t p) c -> p t c", p=P)
                nc.sync.dma_start(out=t[:, win0 // P : (win0 + rows) // P, :], in_=src)

        def add_mask_vector(i, j):
            e = tiles[i]["e"][:, j, :]
            nc.vector.tensor_tensor(out=e, in0=e, in1=mask[steps[i][0]][:, j, :], op=ADD)
            tiles[i]["t", j] = e

        def add_mask_gpsimd(i, half):
            e, m = tiles[i]["e"], mask[steps[i][0]]
            js = slice(2 * half, 2 * half + 2)
            if half == 0:
                t = e[:, js, :]
            else:
                t = work.tile([P, 2, WIN], F32, name="t", tag="v_t%d" % (i % 2) if i > 1 else "dz_t0", bufs=1, align_bytes=64)[:]
            nc.gpsimd.tensor_tensor(out=t, in0=e[:, js, :], in1=m[:, js, :], op=ADD)
            for a in range(2):
                tiles[i]["t", 2 * half + a] = t[:, a, :]

        def exponential(i, j):
            if j % 2 == 0:
                tiles[i]["z", j // 2] = small.tile([P, 2], F32, name="z")
            nc.scalar.activation(
                out=tiles[i]["e"][:, j, :], in_=tiles[i]["t", j], func=EXP, bias=neg_max[:, i, j : j + 1],
                accum_out=tiles[i]["z", j // 2][:, j % 2 : j % 2 + 1],
            )

        def invert(i, half):
            rz = small.tile([P, 2], F32, name="rz", bufs=6)
            nc.vector.reciprocal(out=rz[:], in_=tiles[i]["z", half][:])
            for a in range(2):
                tiles[i]["rz", 2 * half + a] = rz[:, a : a + 1]

        def scale(i, half):
            if half == 0:
                tiles[i]["dz"] = work.tile([P, J, C], BF16, name="dz", align_bytes=64)
            for j in range(2 * half, 2 * half + 2):
                nc.vector.tensor_scalar(
                    out=tiles[i]["dz"][:, j, :].rearrange("p (u x e) -> p u x e", u=2, e=2),
                    in0=tiles[i]["g"][:, j, :].rearrange("p (x u e) -> p u x e", u=2, e=2), scalar1=tiles[i]["rz", j], scalar2=None, op0=MULT
                )

        def staging(i, name):
            t = tiles[i]
            if name not in t:
                t[name] = work.tile([P, J * WIN], BF16, name=name, tag="%s%d" % (name, i % 2), bufs=1, align_bytes=64)
            return t[name]

        def quantise(i, name, a=0, b=2):
            t = tiles[i]
            if a == 0:
                t[name, "q"] = work.tile([P, WIN], U32, name=name + "_q", align_bytes=64)
                t[name, "s"] = work.tile([P, WIN], U8, name=name + "_s", align_bytes=64)
            fmt = E5M2X4 if name in ("dz_t", "dz_il") else E4M3X4
            a, b = a * 2 * P, b * 2 * P
            nc.vector.quantize_mx(out=t[name, "q"][:, a:b].bitcast(fmt), scales=t[name, "s"][:, a:b], in_=t[name][:, J * a : J * b])

        def interleaved(dst, src, cols, run):
            return dict(
                out=dst.rearrange("p (c j) -> p c j", j=J)[:, cols, :].rearrange("p (c i) j -> p c j i", i=run),
                in_=src[:, :, cols].rearrange("p j (c i) -> p c j i", i=run),
            )

        def interleave_e(engine, i, a, b):
            if a < b:
                engine(**interleaved(staging(i, "e_il")[:], tiles[i]["e"], slice(a, b), 4))

        def interleave_dz(engine, i, a, b):
            if a < b:
                engine(**interleaved(staging(i, "dz_il")[:], tiles[i]["dz"], slice(a, b), 4))

        def vector_share(i):
            return {ROWS + 1: VS5}.get(i, VS)

        def scalar_keys(i):
            return {1: K1}.get(i, 0)

        on_vector, on_scalar = nc.vector.tensor_copy, nc.scalar.copy

        def turn(i, name, b, bank):
            words = tiles[i][name][:].rearrange("p a c -> p (a c)").bitcast(F32).rearrange("p (a c) -> p a c", a=J)
            ps = psum.tile([P, 2, 2, P], F32, name="turn", tag=bank)
            tiles[i][name, b] = ps
            for a in range(2):
                for u in range(2):
                    picked = slice(u, C // 2, 2) if name == "v" else slice(u * P, (u + 1) * P)
                    nc.tensor.transpose(ps[:, a, u, :], words[:, 2 * b + a, picked], ident[:])

        def unload(i, name, b):
            dst = staging(i, name + "_t")
            words = dst[:, 2 * J * P * b : 2 * J * P * (b + 1)].bitcast(F32).rearrange("p (a x u) -> p a x u", a=2, u=2)
            nc.scalar.copy(out=words, in_=tiles[i][name, b][:].rearrange("p a u x -> p a x u"))

        def multiply_de(i, j, bank):
            t = tiles[i]
            t["de", j] = psum.tile([P, WIN], F32, name="de", tag=bank)
            cols = slice(P * j, P * (j + 1))
            nc.tensor.matmul_mx(
                out=t["de", j][:], lhsT=t["dz_t", "q"][:, cols].bitcast(E5M2X4), lhsT_scale=t["dz_t", "s"][:, cols],
                rhs=t["v_t", "q"][:].bitcast(E4M3X4), rhs_scale=t["v_t", "s"][:], start=True, stop=True,
            )

        def multiply_dv(i, m, bank):
            t = tiles[i]
            t["dv", m] = psum.tile([P, C], F32, name="dv", tag=bank)
            cols = slice(P * m, P * (m + 1))
            nc.tensor.matmul_mx(
                out=t["dv", m][:], lhsT=t["e_il", "q"][:, cols].bitcast(E4M3X4), lhsT_scale=t["e_il", "s"][:, cols],
                rhs=t["dz_il", "q"][:].bitcast(E5M2X4), rhs_scale=t["dz_il", "s"][:], start=True, stop=True,
            )

        def empty_dv(i, m):
            n, r = steps[i]
            if m == 0:
                tiles[i]["dv_sb"] = work.tile([P, J, C], F32, name="dv_sb", bufs=DVB)
            sb = tiles[i]["dv_sb"]
            nc.scalar.copy(
                out=sb[:, m, :].rearrange("p (x u e) -> p x u e", u=2, e=2),
                in_=tiles[i]["dv", m][:].rearrange("p (u x e) -> p x u e", u=2, e=2),
            )
            count = 1 if i >= last - 1 else 2
            if (m + 1) % count == 0:
                m0 = m + 1 - count
                x0 = [x0 + P * m0 - win0 for win0, x0, rows in spans(n, r) if win0 <= P * m0 < win0 + rows][0]
                dst = image(out_0, r)[x0 : x0 + count * P, :].rearrange("(t p) c -> p t c", p=P)
                nc.sync.dma_start(out=dst, in_=sb[:, m0 : m + 1, :])

        def folded(i, j):
            return steps[i][1] == ROWS - 1 and j < 2

        def weigh(i, j):
            t = tiles[i]
            t["dot", j] = small.tile([P, 1], F32, name="dot", bufs=6)
            t["prod", j] = work.tile([P, WIN], F32, name="prod", tag="prod" if folded(i, j) else "waste")
            nc.vector.scalar_tensor_tensor(
                out=t["prod", j][:], in0=t["de", j][:], scalar=-1.0 if folded(i, j) else t["rz", j], in1=t["e"][:, j, :],
                op0=MULT, op1=MULT, accum_out=t["dot", j][:],
            )

        def subtract(i, j):
            t = tiles[i]
            e = t["e"][:, j, :]
            nc.vector.scalar_tensor_tensor(out=e, in0=t["de", j][:], scalar=t["dot", j][:], in1=e, op0=SUBTRACT, op1=MULT)
            if i < ROWS or j < 2:
                pending.extend((i, j, b) for b in range(2))
                pending.sort(key=lambda x: (x[0] // ROWS, x[1] >= 2, x[0], x[1], x[2]))

        def store_sum(n, j, src):
            nc.sync.dma_start(out=out_1[n].rearrange("(p j) k -> p j k", j=J)[:, j, :], in_=src)

        def sum_next(count=1):
            for i, j, half in pending[:count]:
                n, r = steps[i]
                if r == 0 and half == 0:
                    sums[n, j] = psum.tile([P, WIN], F32, name="sum", tag="sum%d" % j)
                cols = slice(half * WIN // 2, (half + 1) * WIN // 2)
                nc.tensor.matmul(
                    out=sums[n, j][:, cols], lhsT=ident[:], rhs=tiles[i]["e"][:, j, cols],
                    start=(r == 0 and half == 0), stop=(r == ROWS - 1 and half == 1),
                )
            pending[:count] = []

        def sum_product(i, j):
            t = tiles[i]
            assert all(x[1] != j for x in pending)
            nc.tensor.matmul(out=sums[steps[i][0], j][:], lhsT=minus[:], rhs=t["prod", j][:], start=False, stop=True)

        def factor(i, j):
            t = tiles[i]
            t["factor", j] = small.tile([P, 1], F32, name="factor")
            nc.scalar.activation(out=t["factor", j][:], in_=t["dot", j][:], func=COPY, scale=t["rz", j])

        def finish(i, j):
            t = tiles[i]
            e = t["e"][:, j, :]
            nc.vector.scalar_tensor_tensor(out=e, in0=e, scalar=t["factor", j][:], in1=sums[steps[i][0], j][:], op0=MULT, op1=ADD)
            store_sum(steps[i][0], j, e)

        def empty_sum(j):
            assert all(x[1] != j for x in pending if x[0] < ROWS)
            ds = tiles[ROWS - 1]["e"]
            nc.scalar.copy(out=ds[:, j, :], in_=sums[0, j][:])
            store_sum(0, j, ds[:, j, :])

        def add_row_gpsimd(i):
            if i == ROWS + 1:
                total = work.tile([P, 2, WIN], F32, name="total", bufs=1)[:]
                before = tiles[ROWS]["e"][:, 2:J, :]
            else:
                total = work.tile([P, 2, WIN], F32, name="total", tag="dz_il%d" % (last % 2), bufs=1, align_bytes=64)[:]
                before = sums["gpsimd"]
            nc.gpsimd.tensor_tensor(out=total, in0=before, in1=tiles[i]["e"][:, 2:J, :], op=ADD)
            sums["gpsimd"] = total

        def add_last_row(engine, j, a, b):
            ds = tiles[last]["e"][:, j, a:b]
            engine.tensor_tensor(out=ds, in0=sums["gpsimd"][:, j - 2, a:b], in1=ds, op=ADD)
            nc.sync.dma_start(out=out_1[1].rearrange("(p j) k -> p j k", j=J)[:, j, a:b], in_=ds)

        def step(i, op, *args):
            if 0 <= i <= last:
                op(i, *args)

        def forward(s):
            if s == 1:
                scale(1, 0)
                turn(1, "dz", 0, "d")
            else:
                quantise(s, "dz_t", 0, 1)
            scale(s, 1)
            turn(s, "dz", 1, "a")
            if s == 1:
                nc.scalar.activation(out=neg_max[:, 2:ROWS, :], in_=rmax[:, 2:ROWS, 0:J], func=IDENTITY, scale=-1.0)
                exponential(2, 0)
                unload(1, "dz", 0)
                unload(1, "dz", 1)
                exponential(2, 1)
                quantise(1, "v_t")
            else:
                exponential(s + 1, 0)
                exponential(s + 1, 1)
                unload(s, "dz", 1)
            if s == 2:
                negate_row_max(ROWS, 2 * ROWS, nc.vector)
            unload(s + 1, "v", 1)
            interleave_dz(on_vector, s - 1, C - vector_share(s - 1), C)
            interleave_e(on_vector, s, scalar_keys(s), WIN)
            quantise(s - 1, "dz_il")
            if s == 1:
                quantise(s, "dz_t", 0, 1)
            sum_next(2)
            multiply_dv(s - 1, 0, "d")
            multiply_dv(s - 1, 1, "c")
            multiply_de(s, 0, "a")
            multiply_de(s, 1, "b")
            sum_next()
            invert(s + 1, 0)
            quantise(s, "dz_t", 1, 2)
            scale(s + 1, 0)
            interleave_dz(on_scalar, s, 0, P)
            empty_dv(s - 1, 0)
            empty_dv(s - 1, 1)
            turn(s + 1, "dz", 0, "d")
            multiply_de(s, 2, "c")
            quantise(s + 1, "v_t")
            quantise(s, "e_il")

        def backward(s):
            add_mask_gpsimd(s + 1, 1)
            step(s + 2, add_mask_gpsimd, 0)
            if s == last - 1:
                add_row_gpsimd(s - 1)
            fold = folded(s, 0)
            if s == 0:
                interleave_dz(on_scalar, s, EARLY, 3 * P)
                unload(1, "v", 0)
                turn(1, "v", 1, "sum3")
                unload(1, "v", 1)
            else:
                interleave_dz(on_scalar, s, P, 2 * P)
                unload(s + 1, "dz", 0)
            weigh(s, 0)
            if fold:
                sum_next(len([x for x in pending if x[1] < 2]))
                multiply_de(s, 3, "a")
                sum_product(s, 0)
            else:
                sum_next()
            step(s - 1, multiply_dv, 2, "d")
            weigh(s, 1)
            if s == 0:
                invert(1, 0)
            if s:
                interleave_dz(on_scalar, s, 2 * P, C - vector_share(s))
            if fold:
                factor(s, 0)
                factor(s, 1)
            step(s - 1, empty_dv, 2)
            if fold:
                sum_product(s, 1)
                weigh(s, 2)
                weigh(s, 3)
            else:
                subtract(s, 0)
                multiply_de(s, 3, "a")
                weigh(s, 2)
                subtract(s, 1)
                sum_next(2 if s == last - 1 else 1)
            step(s - 1, multiply_dv, 3, "d")
            step(s + 2, turn, "v", 0, "b")
            exponential(s + 1, 2)
            exponential(s + 1, 3)
            if s == 0:
                interleave_e(on_scalar, 1, 0, scalar_keys(1))
                interleave_dz(on_scalar, s, 3 * P, C)
            if fold:
                subtract(s, 2)
                subtract(s, 3)
            else:
                weigh(s, 3)
                subtract(s, 2)
            sum_next(2 if s == last - 1 else 1)
            step(s + 2, turn, "v", 1, "c")
            step(s - 1, empty_dv, 3)
            step(s + 2, unload, "v", 0)
            if s > ROWS:
                empty_sum(s - ROWS + 1)
            if fold:
                finish(s, 0)
                finish(s, 1)
            else:
                subtract(s, 3)
            invert(s + 1, 1)

        def finale(s):
            quantise(s, "dz_t", 0, 1)
            scale(s, 1)
            turn(s, "dz", 1, "a")
            quantise(s - 1, "dz_il")
            sum_next()
            multiply_dv(s - 1, 0, "c")
            multiply_dv(s - 1, 1, "d")
            multiply_dv(s - 1, 2, "b")
            multiply_dv(s - 1, 3, "sum2")
            sum_next(len(pending))
            interleave_dz(on_scalar, s, 0, P)
            unload(s, "dz", 1)
            empty_dv(s - 1, 0)
            interleave_e(on_vector, s, 0, WIN)
            interleave_dz(on_scalar, s, P, C - VL)
            interleave_dz(on_vector, s, C - VL, C)
            for m in range(1, J):
                empty_dv(s - 1, m)
            multiply_de(s, 0, "sum3")
            multiply_de(s, 1, "a")
            quantise(s, "dz_t", 1, 2)
            multiply_de(s, 2, "c")
            quantise(s, "e_il")
            quantise(s, "dz_il")

            add_row_gpsimd(s - 1)
            multiply_dv(s, 0, "d")
            multiply_dv(s, 1, "b")
            weigh(s, 0)
            multiply_de(s, 3, "sum3")
            multiply_dv(s, 2, "sum2")
            sum_product(s, 0)
            empty_dv(s, 0)
            multiply_dv(s, 3, "d")
            weigh(s, 2)
            weigh(s, 1)
            sum_product(s, 1)
            subtract(s, 2)
            empty_dv(s, 1)
            factor(s, 0)
            empty_dv(s, 2)
            factor(s, 1)
            empty_dv(s, 3)
            weigh(s, 3)
            finish(s, 0)
            add_last_row(nc.gpsimd, 2, 0, WIN)
            subtract(s, 3)
            finish(s, 1)
            add_last_row(nc.vector, 3, 0, WIN // 2)
            add_last_row(nc.vector, 3, WIN // 2, WIN)

        make_identity(nc, ident[:])
        with tc.manual_schedule():
            nc.gpsimd.tensor_scalar(out=minus[:], in0=ident[:], scalar1=-1.0, scalar2=0.0, op0=MULT, op1=ADD)
            load_row_max(0, 1, nc.scalar)
            nc.scalar.activation(out=neg_max[:, 0, :], in_=rmax[:, 0, 0:J], func=IDENTITY, scale=-1.0)
            for j in range(J):
                load_scores(0, j, j + 1)
                load_mask(0, j, j + 1)
            load_v(0)
            load_grad(0, 0, 2)
            load_grad(0, 2, J)
            load_row_max(1, 2, nc.sync)
            load_scores(1, 0, 2)
            load_scores(1, 2, J)
            load_scores(2, 0, 2)
            load_v(1)
            load_grad(1, 0, J)
            load_row_max(2, ROWS, nc.sync)
            load_v(2)
            load_grad(2, 0, J)
            load_scores(2, 2, J)
            load_row_max(ROWS, 2 * ROWS, nc.sync)

            for j in range(J):
                add_mask_vector(0, j)
                exponential(0, j)
            turn(0, "v", 0, "c")
            turn(0, "v", 1, "d")
            interleave_e(on_scalar, 0, 0, K0)
            invert(0, 0)
            invert(0, 1)
            interleave_e(on_vector, 0, K0, WIN)
            scale(0, 0)
            turn(0, "dz", 0, "a")
            scale(0, 1)
            turn(0, "dz", 1, "b")
            unload(0, "v", 0)
            unload(0, "v", 1)
            unload(0, "dz", 0)
            nc.scalar.activation(out=neg_max[:, 1, :], in_=rmax[:, 1, 0:J], func=IDENTITY, scale=-1.0)
            unload(0, "dz", 1)
            interleave_dz(on_scalar, 0, 0, EARLY)
            quantise(0, "e_il")
            quantise(0, "v_t")
            quantise(0, "dz_t", 0, 1)
            multiply_de(0, 0, "a")
            multiply_de(0, 1, "b")
            add_mask_vector(1, 0)
            exponential(1, 0)
            quantise(0, "dz_t", 1, 2)
            add_mask_vector(1, 1)
            multiply_de(0, 2, "c")
            exponential(1, 1)
            turn(1, "v", 0, "d")

            for s in range(last):
                if s:
                    step(s + 2, load_v)
                    step(s + 2, load_grad, 0, J)
                step(s + 3, load_scores, 0, J)
                if s == 1:
                    load_mask(1, 0, J)
                if s:
                    forward(s)
                backward(s)
            finale(last)
